import numpy as np
import ml_dtypes


def mxq(x, axis, fmt="e4m3"):
    dtype, down = {"e4m3": (ml_dtypes.float8_e4m3fn, 7), "e5m2": (ml_dtypes.float8_e5m2, 14)}[fmt]
    v = np.moveaxis(np.asarray(x, np.float32).astype(ml_dtypes.bfloat16).astype(np.float64), axis, -1)
    blocks = v.reshape(v.shape[:-1] + (-1, 32))
    amax = np.abs(blocks).max(-1, keepdims=True)
    byte = np.maximum(np.where(amax > 0, np.frexp(amax)[1] - 1 + 127, 0) - down, 1)
    scale = np.exp2(byte - 127.0)
    codes = (blocks / scale).astype(np.float32).astype(dtype).astype(np.float64)
    return np.moveaxis((codes * scale).reshape(v.shape), -1, axis)


WIDE = False


def mx_kscale(k):
    if not WIDE:
        return np.ones(k)
    levels = np.array([10, -10, 5, -5, 0])
    a = np.random.permutation(np.resize(levels, k // 512 * 4)).reshape(k // 512, 4)
    idx = np.arange(k)
    return np.exp2(a[idx // 512, idx % 128 // 32])


BF16 = ml_dtypes.bfloat16


def bf(x):
    return np.asarray(x, np.float32).astype(BF16)


def f64(x):
    return np.asarray(x).astype(np.float64)


B, H, D, DV, N = 1, 4, 512, 512, 1024
DIM = H * DV


def setup_inputs():
    s, t = mx_kscale(N), mx_kscale(D)
    c = np.exp2(np.round(np.log2(s.mean())))
    q = (np.random.standard_normal((B, H, D, N)) - 1.0) * 3.0 / np.sqrt(D) / t[:, None]
    k = (np.random.standard_normal((B, H, D, N)) - 1.0) * 3.0 / np.sqrt(N) * t[:, None] * s
    v = np.random.standard_normal((B, H, DV, N)) * 0.125 * np.sqrt(N) * c / s
    return {"q": bf(q), "k": bf(k), "v": bf(v)}


def reference(q, k, v):
    qr = np.maximum(f64(q), 0.0)
    kr = np.maximum(f64(k), 0.0)
    vk = mxq(f64(v), 3, "e4m3") @ mxq(kr, 3, "e4m3").transpose(0, 1, 3, 2)
    ksum = kr.sum(-1)
    num = mxq(vk, 3, "e4m3") @ mxq(qr, 2, "e4m3")
    den = (ksum[..., None] * qr).sum(-2, keepdims=True)
    out = num / den
    return out.transpose(0, 2, 1, 3).reshape(B, -1, DIM)

@@ -1,0 +1,182 @@
+from contextlib import ExitStack
+
+import concourse.mybir as mybir
+from concourse.masks import make_identity
+
+F32 = mybir.dt.float32
+BF16 = mybir.dt.bfloat16
+U32 = mybir.dt.uint32
+U8 = mybir.dt.uint8
+FP8X4 = mybir.dt.float8_e4m3fn_x4
+ALU = mybir.AluOpType
+ACT = mybir.ActivationFunctionType
+
+P = 128
+PACK = 4
+HEADS = 4
+FEAT = 512
+TOK = 1024
+ROWS = FEAT // P
+PASSES = TOK // (P * PACK)
+BANK = 512
+HALVES = TOK // BANK
+TOK_TILES = TOK // P
+PIECES = 3
+
+FLOPS = 2 * 2 * HEADS * FEAT * FEAT * TOK
+
+
+def tile_relu_linear_att_pa_kernel(tc, q, k, v, out):
+    nc = tc.nc
+    out_view = out[0].rearrange("(j c a) (b n) -> j c a b n", c=ROWS, a=2, b=2)
+
+    with ExitStack() as ctx:
+        consts = ctx.enter_context(tc.tile_pool(name="consts", bufs=1))
+        inputs = ctx.enter_context(tc.tile_pool(name="inputs", bufs=3))
+        work = ctx.enter_context(tc.tile_pool(name="work", bufs=2))
+        stores = ctx.enter_context(tc.tile_pool(name="stores", bufs=4))
+        psum = ctx.enter_context(tc.psum_pool(name="psum", bufs=2))
+        psum_den = ctx.enter_context(tc.psum_pool(name="psum_den", bufs=1))
+
+        ident = consts.tile([P, P], F32)
+        make_identity(nc, ident[:])
+
+        for h in range(HEADS):
+            k_sb = inputs.tile([P, ROWS * TOK], BF16)
+            v_sb = inputs.tile([P, ROWS * TOK], BF16)
+            q_sb = inputs.tile([P, ROWS * TOK], BF16)
+            nc.sync.dma_start(out=k_sb[:], in_=k[0, h].rearrange("(p t) n -> p (t n)", t=ROWS))
+            nc.sync.dma_start(out=v_sb[:], in_=v[0, h].rearrange("(p t) n -> p (t n)", t=ROWS))
+            nc.sync.dma_start(out=q_sb[:], in_=q[0, h].rearrange("(p t) n -> p (t n)", t=ROWS))
+
+            ksum = work.tile([P, ROWS], F32)
+            for t in range(ROWS):
+                row = k_sb[:, t * TOK : (t + 1) * TOK]
+                nc.scalar.activation(out=row, in_=row, func=ACT.Relu, accum_out=ksum[:, t : t + 1])
+
+            ksum3 = work.tile([P, ROWS, PIECES], BF16)
+            rest1 = work.tile([P, ROWS], F32)
+            rest2 = work.tile([P, ROWS], F32)
+            nc.vector.tensor_copy(out=ksum3[:, :, 0], in_=ksum[:])
+            nc.vector.tensor_tensor(out=rest1[:], in0=ksum[:], in1=ksum3[:, :, 0], op=ALU.subtract)
+            nc.vector.tensor_copy(out=ksum3[:, :, 1], in_=rest1[:])
+            nc.vector.tensor_tensor(out=rest2[:], in0=rest1[:], in1=ksum3[:, :, 1], op=ALU.subtract)
+            nc.vector.tensor_copy(out=ksum3[:, :, 2], in_=rest2[:])
+
+            codes = {}
+            scales = {}
+            for name, src in (("k", k_sb), ("v", v_sb)):
+                words = src[:].bitcast(F32)
+                grouped = work.tile([P, PASSES * ROWS * P * PACK], BF16, name="grouped_" + name, align_bytes=64)
+                grouped_words = grouped[:].bitcast(F32)
+                codes[name] = work.tile([P, PASSES * FEAT], U32, name="codes_" + name, align_bytes=64)
+                scales[name] = work.tile([P, PASSES * FEAT], U8, name="scales_" + name, align_bytes=64)
+                for g in range(PASSES):
+                    for pair in range(ROWS // 2):
+                        flipped = psum.tile([P, BANK], F32, name="flipped")
+                        for b in range(2):
+                            for u in range(2):
+                                t = 2 * pair + b
+                                first = t * (TOK // 2) + (2 * g + u) * P
+                                slot = (2 * b + u) * P
+                                nc.tensor.transpose(flipped[:, slot : slot + P], words[:, first : first + P], ident[:])
+                        first = (g * ROWS + 2 * pair) * P * 2
+                        nc.scalar.copy(
+                            out=grouped_words[:, first : first + BANK].rearrange("p (b c u) -> p b c u", b=2, u=2),
+                            in_=flipped[:].rearrange("p (b u c) -> p b c u", b=2, u=2),
+                        )
+                    nc.vector.quantize_mx(
+                        out=codes[name][:, g * FEAT : (g + 1) * FEAT].bitcast(FP8X4),
+                        scales=scales[name][:, g * FEAT : (g + 1) * FEAT],
+                        in_=grouped[:, g * FEAT * PACK : (g + 1) * FEAT * PACK],
+                    )
+
+            nc.vector.tensor_scalar_max(out=q_sb[:], in0=q_sb[:], scalar1=0.0)
+            q_grouped = work.tile([P, TOK * PACK], BF16, align_bytes=64)
+            q_codes = work.tile([P, TOK], U32, align_bytes=64)
+            q_scales = work.tile([P, TOK], U8, align_bytes=64)
+            for half in range(HALVES):
+                nc.vector.tensor_copy(
+                    out=q_grouped[:, half * BANK * PACK : (half + 1) * BANK * PACK].rearrange(
+                        "p (c i t) -> p c t i", i=4, t=PACK
+                    ),
+                    in_=q_sb[:].rearrange("p (t n) -> p t n", t=ROWS)[:, :, half * BANK : (half + 1) * BANK].rearrange(
+                        "p t (c i) -> p c t i", i=4
+                    ),
+                )
+            for half in range(HALVES):
+                nc.vector.quantize_mx(
+                    out=q_codes[:, half * BANK : (half + 1) * BANK].bitcast(FP8X4),
+                    scales=q_scales[:, half * BANK : (half + 1) * BANK],
+                    in_=q_grouped[:, half * BANK * PACK : (half + 1) * BANK * PACK],
+                )
+
+            den_ps = psum_den.tile([P, TOK_TILES, PIECES], F32)
+            for j in range(TOK_TILES):
+                for t in range(ROWS):
+                    nc.tensor.matmul(
+                        out=den_ps[:, j, :],
+                        lhsT=q_sb[:, t * TOK + j * P : t * TOK + (j + 1) * P],
+                        rhs=ksum3[:, t, :],
+                        start=(t == 0),
+                        stop=(t == ROWS - 1),
+                    )
+            den = work.tile([P, TOK_TILES], F32)
+            rden = work.tile([P, TOK_TILES], F32)
+            nc.vector.tensor_reduce(out=den[:], in_=den_ps[:], axis=mybir.AxisListType.X, op=ALU.add)
+            nc.vector.reciprocal(out=rden[:], in_=den[:])
+
+            rden_rows = work.tile([P, TOK], F32)
+            for half in range(HALVES):
+                spread = psum.tile([P, BANK], F32, name="flipped")
+                for jj in range(BANK // P):
+                    j = half * (BANK // P) + jj
+                    nc.tensor.transpose(
+                        spread[:, jj * P : (jj + 1) * P], rden[:, j : j + 1].to_broadcast([P, P]), ident[:]
+                    )
+                nc.scalar.copy(out=rden_rows[:, half * BANK : (half + 1) * BANK], in_=spread[:])
+
+            vk_grouped = work.tile([P, FEAT * PACK], BF16, align_bytes=64)
+            vk_codes = work.tile([P, FEAT], U32, align_bytes=64)
+            vk_scales = work.tile([P, FEAT], U8, align_bytes=64)
+            for c in range(ROWS):
+                vk_ps = psum.tile([P, BANK], F32)
+                for t in range(ROWS):
+                    for g in range(PASSES):
+                        e_cols = slice(g * FEAT + t * P, g * FEAT + (t + 1) * P)
+                        d_cols = slice(g * FEAT + c * P, g * FEAT + (c + 1) * P)
+                        nc.tensor.matmul_mx(
+                            out=vk_ps[:, t * P : (t + 1) * P],
+                            lhsT=codes["k"][:, e_cols].bitcast(FP8X4),
+                            lhsT_scale=scales["k"][:, e_cols],
+                            rhs=codes["v"][:, d_cols].bitcast(FP8X4),
+                            rhs_scale=scales["v"][:, d_cols],
+                            start=(g == 0),
+                            stop=(g == PASSES - 1),
+                        )
+                nc.scalar.copy(
+                    out=vk_grouped[:, c * P * PACK : (c + 1) * P * PACK].rearrange("p (j t) -> p j t", t=PACK),
+                    in_=vk_ps[:].rearrange("p (t j) -> p j t", t=ROWS),
+                )
+                nc.vector.quantize_mx(
+                    out=vk_codes[:, c * P : (c + 1) * P].bitcast(FP8X4),
+                    scales=vk_scales[:, c * P : (c + 1) * P],
+                    in_=vk_grouped[:, c * P * PACK : (c + 1) * P * PACK],
+                )
+
+            for c in range(ROWS):
+                result = stores.tile([P, TOK], F32)
+                for half in range(HALVES):
+                    n_cols = slice(half * BANK, (half + 1) * BANK)
+                    num_ps = psum.tile([P, BANK], F32)
+                    nc.tensor.matmul_mx(
+                        out=num_ps[:],
+                        lhsT=vk_codes[:, c * P : (c + 1) * P].bitcast(FP8X4),
+                        lhsT_scale=vk_scales[:, c * P : (c + 1) * P],
+                        rhs=q_codes[:, n_cols].bitcast(FP8X4),
+                        rhs_scale=q_scales[:, n_cols],
+                        start=True,
+                        stop=True,
+                    )
+                    nc.vector.tensor_tensor(out=result[:, n_cols], in0=num_ps[:], in1=rden_rows[:, n_cols], op=ALU.mult)
+                nc.sync.dma_start(out=out_view[:, c, h // 2, h % 2, :], in_=result[:])

@@ -23,6 +23,11 @@ HALVES = TOK // BANK
 TOK_TILES = TOK // P
 PIECES = 3
 
+QUARTERS = HEADS * ROWS
+EARLY = 6
+AHEAD = 4
+BEHIND = 2
+
 FLOPS = 2 * 2 * HEADS * FEAT * FEAT * TOK
 
 
@@ -32,151 +37,230 @@ def tile_relu_linear_att_pa_kernel(tc, q, k, v, out):
 
     with ExitStack() as ctx:
         consts = ctx.enter_context(tc.tile_pool(name="consts", bufs=1))
-        inputs = ctx.enter_context(tc.tile_pool(name="inputs", bufs=3))
-        work = ctx.enter_context(tc.tile_pool(name="work", bufs=2))
+        inputs = ctx.enter_context(tc.tile_pool(name="inputs", bufs=HEADS))
+        one = ctx.enter_context(tc.tile_pool(name="one", bufs=1))
+        two = ctx.enter_context(tc.tile_pool(name="two", bufs=2))
+        three = ctx.enter_context(tc.tile_pool(name="three", bufs=3))
         stores = ctx.enter_context(tc.tile_pool(name="stores", bufs=4))
-        psum = ctx.enter_context(tc.psum_pool(name="psum", bufs=2))
+        psum_flip = ctx.enter_context(tc.psum_pool(name="psum_flip", bufs=3))
+        psum_mx = ctx.enter_context(tc.psum_pool(name="psum_mx", bufs=2))
         psum_den = ctx.enter_context(tc.psum_pool(name="psum_den", bufs=1))
+        ctx.enter_context(tc.manual_schedule())
 
         ident = consts.tile([P, P], F32)
         make_identity(nc, ident[:])
 
-        for h in range(HEADS):
-            k_sb = inputs.tile([P, ROWS * TOK], BF16)
-            v_sb = inputs.tile([P, ROWS * TOK], BF16)
-            q_sb = inputs.tile([P, ROWS * TOK], BF16)
-            nc.sync.dma_start(out=k_sb[:], in_=k[0, h].rearrange("(p t) n -> p (t n)", t=ROWS))
-            nc.sync.dma_start(out=v_sb[:], in_=v[0, h].rearrange("(p t) n -> p (t n)", t=ROWS))
-            nc.sync.dma_start(out=q_sb[:], in_=q[0, h].rearrange("(p t) n -> p (t n)", t=ROWS))
+        kept = {}
 
-            ksum = work.tile([P, ROWS], F32)
-            for t in range(ROWS):
-                row = k_sb[:, t * TOK : (t + 1) * TOK]
-                nc.scalar.activation(out=row, in_=row, func=ACT.Relu, accum_out=ksum[:, t : t + 1])
+        def load(name, src, h, first_row, n_rows):
+            if first_row == 0:
+                kept[name, h] = inputs.tile([P, ROWS * TOK], BF16, name=name + "_sb")
+            cols = slice(first_row * TOK, (first_row + n_rows) * TOK)
+            nc.sync.dma_start(
+                out=kept[name, h][:, cols], in_=src[0, h].rearrange("(p t) n -> p (t n)", t=ROWS)[:, cols]
+            )
 
-            ksum3 = work.tile([P, ROWS, PIECES], BF16)
-            rest1 = work.tile([P, ROWS], F32)
-            rest2 = work.tile([P, ROWS], F32)
-            nc.vector.tensor_copy(out=ksum3[:, :, 0], in_=ksum[:])
-            nc.vector.tensor_tensor(out=rest1[:], in0=ksum[:], in1=ksum3[:, :, 0], op=ALU.subtract)
-            nc.vector.tensor_copy(out=ksum3[:, :, 1], in_=rest1[:])
-            nc.vector.tensor_tensor(out=rest2[:], in0=rest1[:], in1=ksum3[:, :, 1], op=ALU.subtract)
-            nc.vector.tensor_copy(out=ksum3[:, :, 2], in_=rest2[:])
+        def relu_k(h, t):
+            if t == 0:
+                kept["ksum", h] = two.tile([P, ROWS], F32, name="ksum")
+            row = kept["k", h][:, t * TOK : (t + 1) * TOK]
+            nc.scalar.activation(out=row, in_=row, func=ACT.Relu, accum_out=kept["ksum", h][:, t : t + 1])
 
-            codes = {}
-            scales = {}
-            for name, src in (("k", k_sb), ("v", v_sb)):
-                words = src[:].bitcast(F32)
-                grouped = work.tile([P, PASSES * ROWS * P * PACK], BF16, name="grouped_" + name, align_bytes=64)
-                grouped_words = grouped[:].bitcast(F32)
-                codes[name] = work.tile([P, PASSES * FEAT], U32, name="codes_" + name, align_bytes=64)
-                scales[name] = work.tile([P, PASSES * FEAT], U8, name="scales_" + name, align_bytes=64)
-                for g in range(PASSES):
-                    for pair in range(ROWS // 2):
-                        flipped = psum.tile([P, BANK], F32, name="flipped")
-                        for b in range(2):
-                            for u in range(2):
-                                t = 2 * pair + b
-                                first = t * (TOK // 2) + (2 * g + u) * P
-                                slot = (2 * b + u) * P
-                                nc.tensor.transpose(flipped[:, slot : slot + P], words[:, first : first + P], ident[:])
-                        first = (g * ROWS + 2 * pair) * P * 2
-                        nc.scalar.copy(
-                            out=grouped_words[:, first : first + BANK].rearrange("p (b c u) -> p b c u", b=2, u=2),
-                            in_=flipped[:].rearrange("p (b u c) -> p b c u", b=2, u=2),
-                        )
-                    nc.vector.quantize_mx(
-                        out=codes[name][:, g * FEAT : (g + 1) * FEAT].bitcast(FP8X4),
-                        scales=scales[name][:, g * FEAT : (g + 1) * FEAT],
-                        in_=grouped[:, g * FEAT * PACK : (g + 1) * FEAT * PACK],
-                    )
+        def split_ksum(h):
+            ksum = kept["ksum", h]
+            ksum3 = two.tile([P, ROWS, PIECES], BF16, name="ksum3")
+            rest1 = two.tile([P, ROWS], F32, name="rest1")
+            rest2 = two.tile([P, ROWS], F32, name="rest2")
+            nc.gpsimd.tensor_copy(out=ksum3[:, :, 0], in_=ksum[:])
+            nc.gpsimd.tensor_tensor(out=rest1[:], in0=ksum[:], in1=ksum3[:, :, 0], op=ALU.subtract)
+            nc.gpsimd.tensor_copy(out=ksum3[:, :, 1], in_=rest1[:])
+            nc.gpsimd.tensor_tensor(out=rest2[:], in0=rest1[:], in1=ksum3[:, :, 1], op=ALU.subtract)
+            nc.gpsimd.tensor_copy(out=ksum3[:, :, 2], in_=rest2[:])
+            kept["ksum3", h] = ksum3
 
-            nc.vector.tensor_scalar_max(out=q_sb[:], in0=q_sb[:], scalar1=0.0)
-            q_grouped = work.tile([P, TOK * PACK], BF16, align_bytes=64)
-            q_codes = work.tile([P, TOK], U32, align_bytes=64)
-            q_scales = work.tile([P, TOK], U8, align_bytes=64)
-            for half in range(HALVES):
+        def flip(h, r):
+            name = "kv"[r % 2]
+            pair = r // 2
+            words = kept[name, h][:].bitcast(F32)
+            grouped = three.tile([P, PASSES * 2 * P * PACK], BF16, name="grouped", align_bytes=64)
+            grouped_words = grouped[:].bitcast(F32)
+            for g in range(PASSES):
+                flipped = psum_flip.tile([P, BANK], F32, name="flipped")
+                for b in range(2):
+                    for u in range(2):
+                        first = (2 * pair + b) * (TOK // 2) + (2 * g + u) * P
+                        slot = (2 * b + u) * P
+                        nc.tensor.transpose(flipped[:, slot : slot + P], words[:, first : first + P], ident[:])
+                nc.scalar.copy(
+                    out=grouped_words[:, g * BANK : (g + 1) * BANK].rearrange("p (b c u) -> p b c u", b=2, u=2),
+                    in_=flipped[:].rearrange("p (b u c) -> p b c u", b=2, u=2),
+                )
+            kept["grouped", h, r] = grouped
+
+        def quantise_flipped(h, r):
+            name = "kv"[r % 2]
+            pair = r // 2
+            if pair == 0:
+                kept["codes", name, h] = two.tile([P, PASSES * FEAT], U32, name="codes_" + name, align_bytes=64)
+                kept["scales", name, h] = two.tile([P, PASSES * FEAT], U8, name="scales_" + name, align_bytes=64)
+            width = PASSES * 2 * P
+            nc.vector.quantize_mx(
+                out=kept["codes", name, h][:, pair * width : (pair + 1) * width].bitcast(FP8X4),
+                scales=kept["scales", name, h][:, pair * width : (pair + 1) * width],
+                in_=kept["grouped", h, r][:],
+            )
+
+        def row_block(t, g):
+            first = (((t // 2) * PASSES + g) * 2 + t % 2) * P
+            return slice(first, first + P)
+
+        def q_side(h, part):
+            q_sb = kept["q", h]
+            if part == 0:
+                nc.vector.tensor_scalar_max(out=q_sb[:], in0=q_sb[:], scalar1=0.0)
+                kept["q_grouped", h] = one.tile([P, TOK * PACK], BF16, name="q_grouped", align_bytes=64)
+            elif part <= HALVES:
+                half = part - 1
                 nc.vector.tensor_copy(
-                    out=q_grouped[:, half * BANK * PACK : (half + 1) * BANK * PACK].rearrange(
+                    out=kept["q_grouped", h][:, half * BANK * PACK : (half + 1) * BANK * PACK].rearrange(
                         "p (c i t) -> p c t i", i=4, t=PACK
                     ),
                     in_=q_sb[:].rearrange("p (t n) -> p t n", t=ROWS)[:, :, half * BANK : (half + 1) * BANK].rearrange(
                         "p t (c i) -> p c t i", i=4
                     ),
                 )
-            for half in range(HALVES):
+            else:
+                kept["q_codes", h] = three.tile([P, TOK], U32, name="q_codes", align_bytes=64)
+                kept["q_scales", h] = three.tile([P, TOK], U8, name="q_scales", align_bytes=64)
                 nc.vector.quantize_mx(
-                    out=q_codes[:, half * BANK : (half + 1) * BANK].bitcast(FP8X4),
-                    scales=q_scales[:, half * BANK : (half + 1) * BANK],
-                    in_=q_grouped[:, half * BANK * PACK : (half + 1) * BANK * PACK],
+                    out=kept["q_codes", h][:].bitcast(FP8X4), scales=kept["q_scales", h][:], in_=kept["q_grouped", h][:]
                 )
 
-            den_ps = psum_den.tile([P, TOK_TILES, PIECES], F32)
-            for j in range(TOK_TILES):
+        def den_tiles(h, tiles):
+            for j in tiles:
                 for t in range(ROWS):
                     nc.tensor.matmul(
-                        out=den_ps[:, j, :],
-                        lhsT=q_sb[:, t * TOK + j * P : t * TOK + (j + 1) * P],
-                        rhs=ksum3[:, t, :],
+                        out=kept["den_ps", h][:, j, :],
+                        lhsT=kept["q", h][:, t * TOK + j * P : t * TOK + (j + 1) * P],
+                        rhs=kept["ksum3", h][:, t, :],
                         start=(t == 0),
                         stop=(t == ROWS - 1),
                     )
-            den = work.tile([P, TOK_TILES], F32)
-            rden = work.tile([P, TOK_TILES], F32)
-            nc.vector.tensor_reduce(out=den[:], in_=den_ps[:], axis=mybir.AxisListType.X, op=ALU.add)
-            nc.vector.reciprocal(out=rden[:], in_=den[:])
 
-            rden_rows = work.tile([P, TOK], F32)
+        def reciprocal_den(h):
+            den = two.tile([P, TOK_TILES], F32, name="den")
+            rden = two.tile([P, TOK_TILES], F32, name="rden")
+            nc.vector.tensor_reduce(out=den[:], in_=kept["den_ps", h][:], axis=mybir.AxisListType.X, op=ALU.add)
+            nc.vector.reciprocal(out=rden[:], in_=den[:])
+            kept["rden", h] = rden
+
+        def spread_rden(h):
+            kept["rden_rows", h] = two.tile([P, TOK], F32, name="rden_rows")
             for half in range(HALVES):
-                spread = psum.tile([P, BANK], F32, name="flipped")
+                spread = psum_flip.tile([P, BANK], F32, name="flipped")
                 for jj in range(BANK // P):
                     j = half * (BANK // P) + jj
                     nc.tensor.transpose(
-                        spread[:, jj * P : (jj + 1) * P], rden[:, j : j + 1].to_broadcast([P, P]), ident[:]
+                        spread[:, jj * P : (jj + 1) * P], kept["rden", h][:, j : j + 1].to_broadcast([P, P]), ident[:]
                     )
-                nc.scalar.copy(out=rden_rows[:, half * BANK : (half + 1) * BANK], in_=spread[:])
+                nc.scalar.copy(out=kept["rden_rows", h][:, half * BANK : (half + 1) * BANK], in_=spread[:])
 
-            vk_grouped = work.tile([P, FEAT * PACK], BF16, align_bytes=64)
-            vk_codes = work.tile([P, FEAT], U32, align_bytes=64)
-            vk_scales = work.tile([P, FEAT], U8, align_bytes=64)
-            for c in range(ROWS):
-                vk_ps = psum.tile([P, BANK], F32)
-                for t in range(ROWS):
-                    for g in range(PASSES):
-                        e_cols = slice(g * FEAT + t * P, g * FEAT + (t + 1) * P)
-                        d_cols = slice(g * FEAT + c * P, g * FEAT + (c + 1) * P)
-                        nc.tensor.matmul_mx(
-                            out=vk_ps[:, t * P : (t + 1) * P],
-                            lhsT=codes["k"][:, e_cols].bitcast(FP8X4),
-                            lhsT_scale=scales["k"][:, e_cols],
-                            rhs=codes["v"][:, d_cols].bitcast(FP8X4),
-                            rhs_scale=scales["v"][:, d_cols],
-                            start=(g == 0),
-                            stop=(g == PASSES - 1),
-                        )
-                nc.scalar.copy(
-                    out=vk_grouped[:, c * P * PACK : (c + 1) * P * PACK].rearrange("p (j t) -> p j t", t=PACK),
-                    in_=vk_ps[:].rearrange("p (t j) -> p j t", t=ROWS),
-                )
-                nc.vector.quantize_mx(
-                    out=vk_codes[:, c * P : (c + 1) * P].bitcast(FP8X4),
-                    scales=vk_scales[:, c * P : (c + 1) * P],
-                    in_=vk_grouped[:, c * P * PACK : (c + 1) * P * PACK],
-                )
-
-            for c in range(ROWS):
-                result = stores.tile([P, TOK], F32)
-                for half in range(HALVES):
-                    n_cols = slice(half * BANK, (half + 1) * BANK)
-                    num_ps = psum.tile([P, BANK], F32)
+        def first_matmul(h, c):
+            vk_ps = psum_mx.tile([P, BANK], F32, name="vk_ps")
+            for t in range(ROWS):
+                for g in range(PASSES):
                     nc.tensor.matmul_mx(
-                        out=num_ps[:],
-                        lhsT=vk_codes[:, c * P : (c + 1) * P].bitcast(FP8X4),
-                        lhsT_scale=vk_scales[:, c * P : (c + 1) * P],
-                        rhs=q_codes[:, n_cols].bitcast(FP8X4),
-                        rhs_scale=q_scales[:, n_cols],
-                        start=True,
-                        stop=True,
+                        out=vk_ps[:, t * P : (t + 1) * P],
+                        lhsT=kept["codes", "k", h][:, row_block(t, g)].bitcast(FP8X4),
+                        lhsT_scale=kept["scales", "k", h][:, row_block(t, g)],
+                        rhs=kept["codes", "v", h][:, row_block(c, g)].bitcast(FP8X4),
+                        rhs_scale=kept["scales", "v", h][:, row_block(c, g)],
+                        start=(g == 0),
+                        stop=(g == PASSES - 1),
                     )
-                    nc.vector.tensor_tensor(out=result[:, n_cols], in0=num_ps[:], in1=rden_rows[:, n_cols], op=ALU.mult)
-                nc.sync.dma_start(out=out_view[:, c, h // 2, h % 2, :], in_=result[:])
+            kept["vk_ps", h, c] = vk_ps
+
+        def round_vk(h, c):
+            vk_grouped = three.tile([P, P * PACK], BF16, name="vk_grouped", align_bytes=64)
+            nc.scalar.copy(
+                out=vk_grouped[:].rearrange("p (j t) -> p j t", t=PACK),
+                in_=kept["vk_ps", h, c][:].rearrange("p (t j) -> p j t", t=ROWS),
+            )
+            kept["vk_grouped", h, c] = vk_grouped
+
+        def quantise_vk(h, c):
+            kept["vk_codes", h, c] = three.tile([P, P], U32, name="vk_codes", align_bytes=64)
+            kept["vk_scales", h, c] = three.tile([P, P], U8, name="vk_scales", align_bytes=64)
+            nc.vector.quantize_mx(
+                out=kept["vk_codes", h, c][:].bitcast(FP8X4),
+                scales=kept["vk_scales", h, c][:],
+                in_=kept["vk_grouped", h, c][:],
+            )
+
+        def second_matmul(h, c):
+            for half in range(HALVES):
+                n_cols = slice(half * BANK, (half + 1) * BANK)
+                num_ps = psum_mx.tile([P, BANK], F32, name="num_ps")
+                nc.tensor.matmul_mx(
+                    out=num_ps[:],
+                    lhsT=kept["vk_codes", h, c][:].bitcast(FP8X4),
+                    lhsT_scale=kept["vk_scales", h, c][:],
+                    rhs=kept["q_codes", h][:, n_cols].bitcast(FP8X4),
+                    rhs_scale=kept["q_scales", h][:, n_cols],
+                    start=True,
+                    stop=True,
+                )
+                kept["num_ps", h, c, half] = num_ps
+
+        def divide_and_store(h, c):
+            result = stores.tile([P, TOK], F32, name="result")
+            for half in range(HALVES):
+                n_cols = slice(half * BANK, (half + 1) * BANK)
+                nc.vector.tensor_tensor(
+                    out=result[:, n_cols], in0=kept["num_ps", h, c, half][:], in1=kept["rden_rows", h][:, n_cols], op=ALU.mult
+                )
+            nc.sync.dma_start(out=out_view[:, c, h // 2, h % 2, :], in_=result[:])
+
+        load("k", k, 0, 0, 2)
+        load("k", k, 0, 2, 2)
+        load("v", v, 0, 0, 2)
+        load("q", q, 0, 0, ROWS)
+        load("v", v, 0, 2, 2)
+        for h in range(1, HEADS):
+            load("k", k, h, 0, ROWS)
+            load("q", q, h, 0, ROWS)
+            load("v", v, h, 0, ROWS)
+
+        def valid(s):
+            return 0 <= s < QUARTERS
+
+        for step in range(-EARLY, QUARTERS + BEHIND):
+            if valid(step) and step % ROWS == 1:
+                reciprocal_den(step // ROWS)
+            if valid(step + AHEAD):
+                flip((step + AHEAD) // ROWS, (step + AHEAD) % ROWS)
+            if valid(step + AHEAD - 1):
+                quantise_flipped((step + AHEAD - 1) // ROWS, (step + AHEAD - 1) % ROWS)
+            if valid(step - BEHIND):
+                second_matmul((step - BEHIND) // ROWS, (step - BEHIND) % ROWS)
+            if valid(step - 1):
+                quantise_vk((step - 1) // ROWS, (step - 1) % ROWS)
+            if valid(step + EARLY):
+                relu_k((step + EARLY) // ROWS, (step + EARLY) % ROWS)
+                if (step + EARLY) % ROWS == ROWS - 1:
+                    split_ksum((step + EARLY) // ROWS)
+            if valid(step):
+                first_matmul(step // ROWS, step % ROWS)
+            if valid(step + EARLY):
+                q_side((step + EARLY) // ROWS, (step + EARLY) % ROWS)
+            if valid(step):
+                round_vk(step // ROWS, step % ROWS)
+            if valid(step) and step % ROWS == 1:
+                spread_rden(step // ROWS)
+            if valid(step + 1) and (step + 1) % ROWS == 0:
+                kept["den_ps", (step + 1) // ROWS] = psum_den.tile([P, TOK_TILES, PIECES], F32, name="den_ps")
+                den_tiles((step + 1) // ROWS, range(0, TOK_TILES // 2))
+            if valid(step) and step % ROWS == 0:
+                den_tiles(step // ROWS, range(TOK_TILES // 2, TOK_TILES))
+            if valid(step - BEHIND):
+                divide_and_store((step - BEHIND) // ROWS, (step - BEHIND) % ROWS)

@@ -24,7 +24,7 @@ TOK_TILES = TOK // P
 PIECES = 3
 
 QUARTERS = HEADS * ROWS
-EARLY = 6
+EARLY = 7
 AHEAD = 4
 BEHIND = 2
 
@@ -42,8 +42,7 @@ def tile_relu_linear_att_pa_kernel(tc, q, k, v, out):
         two = ctx.enter_context(tc.tile_pool(name="two", bufs=2))
         three = ctx.enter_context(tc.tile_pool(name="three", bufs=3))
         stores = ctx.enter_context(tc.tile_pool(name="stores", bufs=4))
-        psum_flip = ctx.enter_context(tc.psum_pool(name="psum_flip", bufs=3))
-        psum_mx = ctx.enter_context(tc.psum_pool(name="psum_mx", bufs=2))
+        psum = ctx.enter_context(tc.psum_pool(name="psum", bufs=7))
         psum_den = ctx.enter_context(tc.psum_pool(name="psum_den", bufs=1))
         ctx.enter_context(tc.manual_schedule())
 
@@ -85,7 +84,7 @@ def tile_relu_linear_att_pa_kernel(tc, q, k, v, out):
             grouped = three.tile([P, PASSES * 2 * P * PACK], BF16, name="grouped", align_bytes=64)
             grouped_words = grouped[:].bitcast(F32)
             for g in range(PASSES):
-                flipped = psum_flip.tile([P, BANK], F32, name="flipped")
+                flipped = psum.tile([P, BANK], F32, name="flipped", tag="bank")
                 for b in range(2):
                     for u in range(2):
                         first = (2 * pair + b) * (TOK // 2) + (2 * g + u) * P
@@ -157,7 +156,7 @@ def tile_relu_linear_att_pa_kernel(tc, q, k, v, out):
         def spread_rden(h):
             kept["rden_rows", h] = two.tile([P, TOK], F32, name="rden_rows")
             for half in range(HALVES):
-                spread = psum_flip.tile([P, BANK], F32, name="flipped")
+                spread = psum.tile([P, BANK], F32, name="spread", tag="bank")
                 for jj in range(BANK // P):
                     j = half * (BANK // P) + jj
                     nc.tensor.transpose(
@@ -166,7 +165,7 @@ def tile_relu_linear_att_pa_kernel(tc, q, k, v, out):
                 nc.scalar.copy(out=kept["rden_rows", h][:, half * BANK : (half + 1) * BANK], in_=spread[:])
 
         def first_matmul(h, c):
-            vk_ps = psum_mx.tile([P, BANK], F32, name="vk_ps")
+            vk_ps = psum.tile([P, BANK], F32, name="vk_ps", tag="bank")
             for t in range(ROWS):
                 for g in range(PASSES):
                     nc.tensor.matmul_mx(
@@ -200,7 +199,7 @@ def tile_relu_linear_att_pa_kernel(tc, q, k, v, out):
         def second_matmul(h, c):
             for half in range(HALVES):
                 n_cols = slice(half * BANK, (half + 1) * BANK)
-                num_ps = psum_mx.tile([P, BANK], F32, name="num_ps")
+                num_ps = psum.tile([P, BANK], F32, name="num_ps", tag="bank")
                 nc.tensor.matmul_mx(
                     out=num_ps[:],
                     lhsT=kept["vk_codes", h, c][:].bitcast(FP8X4),

@@ -23,10 +23,10 @@ HALVES = TOK // BANK
 TOK_TILES = TOK // P
 PIECES = 3
 
-QUARTERS = HEADS * ROWS
 EARLY = 7
 AHEAD = 4
 BEHIND = 2
+QUARTERS = HEADS * ROWS
 
 FLOPS = 2 * 2 * HEADS * FEAT * FEAT * TOK
 
@@ -38,22 +38,22 @@ def tile_relu_linear_att_pa_kernel(tc, q, k, v, out):
     with ExitStack() as ctx:
         consts = ctx.enter_context(tc.tile_pool(name="consts", bufs=1))
         inputs = ctx.enter_context(tc.tile_pool(name="inputs", bufs=HEADS))
-        one = ctx.enter_context(tc.tile_pool(name="one", bufs=1))
-        two = ctx.enter_context(tc.tile_pool(name="two", bufs=2))
-        three = ctx.enter_context(tc.tile_pool(name="three", bufs=3))
-        stores = ctx.enter_context(tc.tile_pool(name="stores", bufs=4))
+        single = ctx.enter_context(tc.tile_pool(name="single", bufs=1))
+        double = ctx.enter_context(tc.tile_pool(name="double", bufs=2))
+        triple = ctx.enter_context(tc.tile_pool(name="triple", bufs=3))
+        results = ctx.enter_context(tc.tile_pool(name="results", bufs=6))
         psum = ctx.enter_context(tc.psum_pool(name="psum", bufs=7))
         psum_den = ctx.enter_context(tc.psum_pool(name="psum_den", bufs=1))
         ctx.enter_context(tc.manual_schedule())
 
-        ident = consts.tile([P, P], F32)
-        make_identity(nc, ident[:])
+        identity = consts.tile([P, P], F32)
+        make_identity(nc, identity[:])
 
         kept = {}
 
         def load(name, src, h, first_row, n_rows):
             if first_row == 0:
-                kept[name, h] = inputs.tile([P, ROWS * TOK], BF16, name=name + "_sb")
+                kept[name, h] = inputs.tile([P, ROWS * TOK], BF16, name=name + "_rows")
             cols = slice(first_row * TOK, (first_row + n_rows) * TOK)
             nc.sync.dma_start(
                 out=kept[name, h][:, cols], in_=src[0, h].rearrange("(p t) n -> p (t n)", t=ROWS)[:, cols]
@@ -61,106 +61,106 @@ def tile_relu_linear_att_pa_kernel(tc, q, k, v, out):
 
         def relu_k(h, t):
             if t == 0:
-                kept["ksum", h] = two.tile([P, ROWS], F32, name="ksum")
+                kept["ksum", h] = double.tile([P, ROWS], F32, name="ksum")
             row = kept["k", h][:, t * TOK : (t + 1) * TOK]
             nc.scalar.activation(out=row, in_=row, func=ACT.Relu, accum_out=kept["ksum", h][:, t : t + 1])
 
         def split_ksum(h):
             ksum = kept["ksum", h]
-            ksum3 = two.tile([P, ROWS, PIECES], BF16, name="ksum3")
-            rest1 = two.tile([P, ROWS], F32, name="rest1")
-            rest2 = two.tile([P, ROWS], F32, name="rest2")
-            nc.gpsimd.tensor_copy(out=ksum3[:, :, 0], in_=ksum[:])
-            nc.gpsimd.tensor_tensor(out=rest1[:], in0=ksum[:], in1=ksum3[:, :, 0], op=ALU.subtract)
-            nc.gpsimd.tensor_copy(out=ksum3[:, :, 1], in_=rest1[:])
-            nc.gpsimd.tensor_tensor(out=rest2[:], in0=rest1[:], in1=ksum3[:, :, 1], op=ALU.subtract)
-            nc.gpsimd.tensor_copy(out=ksum3[:, :, 2], in_=rest2[:])
-            kept["ksum3", h] = ksum3
+            pieces = double.tile([P, ROWS, PIECES], BF16, name="ksum_pieces")
+            rest1 = double.tile([P, ROWS], F32, name="rest1")
+            rest2 = double.tile([P, ROWS], F32, name="rest2")
+            nc.gpsimd.tensor_copy(out=pieces[:, :, 0], in_=ksum[:])
+            nc.gpsimd.tensor_tensor(out=rest1[:], in0=ksum[:], in1=pieces[:, :, 0], op=ALU.subtract)
+            nc.gpsimd.tensor_copy(out=pieces[:, :, 1], in_=rest1[:])
+            nc.gpsimd.tensor_tensor(out=rest2[:], in0=rest1[:], in1=pieces[:, :, 1], op=ALU.subtract)
+            nc.gpsimd.tensor_copy(out=pieces[:, :, 2], in_=rest2[:])
+            kept["ksum_pieces", h] = pieces
 
-        def flip(h, r):
-            name = "kv"[r % 2]
-            pair = r // 2
+        def transpose_rows(h, run):
+            name = "k" if run % 2 == 0 else "v"
+            pair = run // 2
             words = kept[name, h][:].bitcast(F32)
-            grouped = three.tile([P, PASSES * 2 * P * PACK], BF16, name="grouped", align_bytes=64)
+            grouped = triple.tile([P, PASSES * 2 * P * PACK], BF16, name="grouped", align_bytes=64)
             grouped_words = grouped[:].bitcast(F32)
             for g in range(PASSES):
                 flipped = psum.tile([P, BANK], F32, name="flipped", tag="bank")
                 for b in range(2):
                     for u in range(2):
                         first = (2 * pair + b) * (TOK // 2) + (2 * g + u) * P
-                        slot = (2 * b + u) * P
-                        nc.tensor.transpose(flipped[:, slot : slot + P], words[:, first : first + P], ident[:])
+                        block = (2 * b + u) * P
+                        nc.tensor.transpose(flipped[:, block : block + P], words[:, first : first + P], identity[:])
                 nc.scalar.copy(
                     out=grouped_words[:, g * BANK : (g + 1) * BANK].rearrange("p (b c u) -> p b c u", b=2, u=2),
                     in_=flipped[:].rearrange("p (b u c) -> p b c u", b=2, u=2),
                 )
-            kept["grouped", h, r] = grouped
+            kept["grouped", h, run] = grouped
 
-        def quantise_flipped(h, r):
-            name = "kv"[r % 2]
-            pair = r // 2
+        def quantise_rows(h, run):
+            name = "k" if run % 2 == 0 else "v"
+            pair = run // 2
             if pair == 0:
-                kept["codes", name, h] = two.tile([P, PASSES * FEAT], U32, name="codes_" + name, align_bytes=64)
-                kept["scales", name, h] = two.tile([P, PASSES * FEAT], U8, name="scales_" + name, align_bytes=64)
+                kept["codes", name, h] = double.tile([P, PASSES * FEAT], U32, name="codes_" + name, align_bytes=64)
+                kept["scales", name, h] = double.tile([P, PASSES * FEAT], U8, name="scales_" + name, align_bytes=64)
             width = PASSES * 2 * P
             nc.vector.quantize_mx(
                 out=kept["codes", name, h][:, pair * width : (pair + 1) * width].bitcast(FP8X4),
                 scales=kept["scales", name, h][:, pair * width : (pair + 1) * width],
-                in_=kept["grouped", h, r][:],
+                in_=kept["grouped", h, run][:],
             )
 
         def row_block(t, g):
             first = (((t // 2) * PASSES + g) * 2 + t % 2) * P
             return slice(first, first + P)
 
-        def q_side(h, part):
-            q_sb = kept["q", h]
+        def prepare_q(h, part):
+            q_rows = kept["q", h]
             if part == 0:
-                nc.vector.tensor_scalar_max(out=q_sb[:], in0=q_sb[:], scalar1=0.0)
-                kept["q_grouped", h] = one.tile([P, TOK * PACK], BF16, name="q_grouped", align_bytes=64)
+                nc.vector.tensor_scalar_max(out=q_rows[:], in0=q_rows[:], scalar1=0.0)
+                kept["q_grouped", h] = single.tile([P, TOK * PACK], BF16, name="q_grouped", align_bytes=64)
             elif part <= HALVES:
                 half = part - 1
                 nc.vector.tensor_copy(
                     out=kept["q_grouped", h][:, half * BANK * PACK : (half + 1) * BANK * PACK].rearrange(
                         "p (c i t) -> p c t i", i=4, t=PACK
                     ),
-                    in_=q_sb[:].rearrange("p (t n) -> p t n", t=ROWS)[:, :, half * BANK : (half + 1) * BANK].rearrange(
+                    in_=q_rows[:].rearrange("p (t n) -> p t n", t=ROWS)[:, :, half * BANK : (half + 1) * BANK].rearrange(
                         "p t (c i) -> p c t i", i=4
                     ),
                 )
             else:
-                kept["q_codes", h] = three.tile([P, TOK], U32, name="q_codes", align_bytes=64)
-                kept["q_scales", h] = three.tile([P, TOK], U8, name="q_scales", align_bytes=64)
+                kept["q_codes", h] = triple.tile([P, TOK], U32, name="q_codes", align_bytes=64)
+                kept["q_scales", h] = triple.tile([P, TOK], U8, name="q_scales", align_bytes=64)
                 nc.vector.quantize_mx(
                     out=kept["q_codes", h][:].bitcast(FP8X4), scales=kept["q_scales", h][:], in_=kept["q_grouped", h][:]
                 )
 
-        def den_tiles(h, tiles):
+        def den_matmuls(h, tiles):
             for j in tiles:
                 for t in range(ROWS):
                     nc.tensor.matmul(
                         out=kept["den_ps", h][:, j, :],
                         lhsT=kept["q", h][:, t * TOK + j * P : t * TOK + (j + 1) * P],
-                        rhs=kept["ksum3", h][:, t, :],
+                        rhs=kept["ksum_pieces", h][:, t, :],
                         start=(t == 0),
                         stop=(t == ROWS - 1),
                     )
 
         def reciprocal_den(h):
-            den = two.tile([P, TOK_TILES], F32, name="den")
-            rden = two.tile([P, TOK_TILES], F32, name="rden")
+            den = double.tile([P, TOK_TILES], F32, name="den")
+            rden = double.tile([P, TOK_TILES], F32, name="rden")
             nc.vector.tensor_reduce(out=den[:], in_=kept["den_ps", h][:], axis=mybir.AxisListType.X, op=ALU.add)
             nc.vector.reciprocal(out=rden[:], in_=den[:])
             kept["rden", h] = rden
 
         def spread_rden(h):
-            kept["rden_rows", h] = two.tile([P, TOK], F32, name="rden_rows")
+            kept["rden_rows", h] = double.tile([P, TOK], F32, name="rden_rows")
             for half in range(HALVES):
                 spread = psum.tile([P, BANK], F32, name="spread", tag="bank")
                 for jj in range(BANK // P):
                     j = half * (BANK // P) + jj
                     nc.tensor.transpose(
-                        spread[:, jj * P : (jj + 1) * P], kept["rden", h][:, j : j + 1].to_broadcast([P, P]), ident[:]
+                        spread[:, jj * P : (jj + 1) * P], kept["rden", h][:, j : j + 1].to_broadcast([P, P]), identity[:]
                     )
                 nc.scalar.copy(out=kept["rden_rows", h][:, half * BANK : (half + 1) * BANK], in_=spread[:])
 
@@ -180,7 +180,7 @@ def tile_relu_linear_att_pa_kernel(tc, q, k, v, out):
             kept["vk_ps", h, c] = vk_ps
 
         def round_vk(h, c):
-            vk_grouped = three.tile([P, P * PACK], BF16, name="vk_grouped", align_bytes=64)
+            vk_grouped = triple.tile([P, P * PACK], BF16, name="vk_grouped", align_bytes=64)
             nc.scalar.copy(
                 out=vk_grouped[:].rearrange("p (j t) -> p j t", t=PACK),
                 in_=kept["vk_ps", h, c][:].rearrange("p (t j) -> p j t", t=ROWS),
@@ -188,8 +188,8 @@ def tile_relu_linear_att_pa_kernel(tc, q, k, v, out):
             kept["vk_grouped", h, c] = vk_grouped
 
         def quantise_vk(h, c):
-            kept["vk_codes", h, c] = three.tile([P, P], U32, name="vk_codes", align_bytes=64)
-            kept["vk_scales", h, c] = three.tile([P, P], U8, name="vk_scales", align_bytes=64)
+            kept["vk_codes", h, c] = triple.tile([P, P], U32, name="vk_codes", align_bytes=64)
+            kept["vk_scales", h, c] = triple.tile([P, P], U8, name="vk_scales", align_bytes=64)
             nc.vector.quantize_mx(
                 out=kept["vk_codes", h, c][:].bitcast(FP8X4),
                 scales=kept["vk_scales", h, c][:],
@@ -212,54 +212,54 @@ def tile_relu_linear_att_pa_kernel(tc, q, k, v, out):
                 kept["num_ps", h, c, half] = num_ps
 
         def divide_and_store(h, c):
-            result = stores.tile([P, TOK], F32, name="result")
             for half in range(HALVES):
                 n_cols = slice(half * BANK, (half + 1) * BANK)
+                result = results.tile([P, BANK], F32, name="result")
                 nc.vector.tensor_tensor(
-                    out=result[:, n_cols], in0=kept["num_ps", h, c, half][:], in1=kept["rden_rows", h][:, n_cols], op=ALU.mult
+                    out=result[:], in0=kept["num_ps", h, c, half][:], in1=kept["rden_rows", h][:, n_cols], op=ALU.mult
                 )
-            nc.sync.dma_start(out=out_view[:, c, h // 2, h % 2, :], in_=result[:])
+                nc.sync.dma_start(out=out_view[:, c, h // 2, h % 2, n_cols], in_=result[:])
 
-        load("k", k, 0, 0, 2)
-        load("k", k, 0, 2, 2)
-        load("v", v, 0, 0, 2)
+        for t in range(ROWS):
+            load("k", k, 0, t, 1)
+        load("v", v, 0, 0, ROWS // 2)
         load("q", q, 0, 0, ROWS)
-        load("v", v, 0, 2, 2)
+        load("v", v, 0, ROWS // 2, ROWS // 2)
         for h in range(1, HEADS):
             load("k", k, h, 0, ROWS)
             load("q", q, h, 0, ROWS)
             load("v", v, h, 0, ROWS)
 
-        def valid(s):
-            return 0 <= s < QUARTERS
+        def valid(quarter):
+            return 0 <= quarter < QUARTERS
 
         for step in range(-EARLY, QUARTERS + BEHIND):
             if valid(step) and step % ROWS == 1:
                 reciprocal_den(step // ROWS)
             if valid(step + AHEAD):
-                flip((step + AHEAD) // ROWS, (step + AHEAD) % ROWS)
+                transpose_rows(*divmod(step + AHEAD, ROWS))
             if valid(step + AHEAD - 1):
-                quantise_flipped((step + AHEAD - 1) // ROWS, (step + AHEAD - 1) % ROWS)
+                quantise_rows(*divmod(step + AHEAD - 1, ROWS))
             if valid(step - BEHIND):
-                second_matmul((step - BEHIND) // ROWS, (step - BEHIND) % ROWS)
+                second_matmul(*divmod(step - BEHIND, ROWS))
             if valid(step - 1):
-                quantise_vk((step - 1) // ROWS, (step - 1) % ROWS)
+                quantise_vk(*divmod(step - 1, ROWS))
             if valid(step + EARLY):
-                relu_k((step + EARLY) // ROWS, (step + EARLY) % ROWS)
+                relu_k(*divmod(step + EARLY, ROWS))
                 if (step + EARLY) % ROWS == ROWS - 1:
                     split_ksum((step + EARLY) // ROWS)
             if valid(step):
-                first_matmul(step // ROWS, step % ROWS)
+                first_matmul(*divmod(step, ROWS))
             if valid(step + EARLY):
-                q_side((step + EARLY) // ROWS, (step + EARLY) % ROWS)
+                prepare_q(*divmod(step + EARLY, ROWS))
             if valid(step):
-                round_vk(step // ROWS, step % ROWS)
+                round_vk(*divmod(step, ROWS))
             if valid(step) and step % ROWS == 1:
                 spread_rden(step // ROWS)
             if valid(step + 1) and (step + 1) % ROWS == 0:
                 kept["den_ps", (step + 1) // ROWS] = psum_den.tile([P, TOK_TILES, PIECES], F32, name="den_ps")
-                den_tiles((step + 1) // ROWS, range(0, TOK_TILES // 2))
+                den_matmuls((step + 1) // ROWS, range(0, TOK_TILES // 2))
             if valid(step) and step % ROWS == 0:
-                den_tiles(step // ROWS, range(TOK_TILES // 2, TOK_TILES))
+                den_matmuls(step // ROWS, range(TOK_TILES // 2, TOK_TILES))
             if valid(step - BEHIND):
-                divide_and_store((step - BEHIND) // ROWS, (step - BEHIND) % ROWS)
+                divide_and_store(*divmod(step - BEHIND, ROWS))

@@ -22,10 +22,22 @@ BANK = 512
 HALVES = TOK // BANK
 TOK_TILES = TOK // P
 PIECES = 3
+SMALL = ROWS + TOK_TILES * PIECES
+Q_CHUNK = TOK // ROWS
 
-EARLY = 7
-AHEAD = 4
+RELU_AHEAD = 7
+K_AHEAD = 6
+KSUM_AHEAD = 5
+Q_AHEAD = 4
+V_AHEAD = 3
 BEHIND = 2
+DEN_STEPS = (0, 0)
+RDEN_STEP = 0
+QQ_STEP = 1
+S_CHUNKS = ((0, 2), (0, 2), (0, 2), (0, 2))
+RELU_LATE = False
+K_LATE = 0
+LOADS = "k00 k01 k02 k03 q0 v001 k101 v023 k123 q1 v101 k201 v123 k223 q2 v2 k3 q3 v3"
 QUARTERS = HEADS * ROWS
 
 FLOPS = 2 * 2 * HEADS * FEAT * FEAT * TOK
@@ -38,38 +50,109 @@ def tile_relu_linear_att_pa_kernel(tc, q, k, v, out):
     with ExitStack() as ctx:
         consts = ctx.enter_context(tc.tile_pool(name="consts", bufs=1))
         inputs = ctx.enter_context(tc.tile_pool(name="inputs", bufs=HEADS))
-        single = ctx.enter_context(tc.tile_pool(name="single", bufs=1))
         double = ctx.enter_context(tc.tile_pool(name="double", bufs=2))
         triple = ctx.enter_context(tc.tile_pool(name="triple", bufs=3))
+        codes_pool = ctx.enter_context(tc.tile_pool(name="codes_pool", bufs=11))
         results = ctx.enter_context(tc.tile_pool(name="results", bufs=6))
         psum = ctx.enter_context(tc.psum_pool(name="psum", bufs=7))
-        psum_den = ctx.enter_context(tc.psum_pool(name="psum_den", bufs=1))
+        psum_small = ctx.enter_context(tc.psum_pool(name="psum_small", bufs=1))
         ctx.enter_context(tc.manual_schedule())
 
         identity = consts.tile([P, P], F32)
         make_identity(nc, identity[:])
+        ones = consts.tile([P, 1], BF16)
+        nc.gpsimd.memset(ones[:], 1.0)
+        small = psum_small.tile([P, 2 * SMALL], F32, name="small")
 
         kept = {}
 
-        def load(name, src, h, first_row, n_rows):
-            if first_row == 0:
+        def load(name, src, h, rows, cols):
+            if (name, h) not in kept:
                 kept[name, h] = inputs.tile([P, ROWS * TOK], BF16, name=name + "_rows")
-            cols = slice(first_row * TOK, (first_row + n_rows) * TOK)
             nc.sync.dma_start(
-                out=kept[name, h][:, cols], in_=src[0, h].rearrange("(p t) n -> p (t n)", t=ROWS)[:, cols]
+                out=kept[name, h][:].rearrange("p (t n) -> p t n", t=ROWS)[:, rows, cols],
+                in_=src[0, h].rearrange("(p t) n -> p t n", t=ROWS)[:, rows, cols],
             )
 
+        def ksum_ps(h):
+            first = (h % 2) * SMALL
+            return small[:, first : first + ROWS]
+
+        def den_ps(h):
+            first = (h % 2) * SMALL + ROWS
+            return small[:, first : first + TOK_TILES * PIECES].rearrange("p (j i) -> p j i", i=PIECES)
+
         def relu_k(h, t):
-            if t == 0:
-                kept["ksum", h] = double.tile([P, ROWS], F32, name="ksum")
             row = kept["k", h][:, t * TOK : (t + 1) * TOK]
-            nc.scalar.activation(out=row, in_=row, func=ACT.Relu, accum_out=kept["ksum", h][:, t : t + 1])
+            nc.vector.tensor_scalar_max(out=row, in0=row, scalar1=0.0)
+
+        def transpose_row(name, h, t):
+            words = kept[name, h][:].bitcast(F32)
+            flipped = psum.tile([P, BANK], F32, name="flipped", tag="bank")
+            for b in range(ROWS):
+                first = t * (TOK // 2) + b * P
+                nc.tensor.transpose(flipped[:, b * P : (b + 1) * P], words[:, first : first + P], identity[:])
+            return flipped
+
+        def group_row(flipped, grouped, side):
+            nc.scalar.copy(
+                out=grouped[:].bitcast(F32)[:, side * BANK : (side + 1) * BANK].rearrange(
+                    "p (g c u) -> p g c u", g=PASSES, u=2
+                ),
+                in_=flipped[:].rearrange("p (g u c) -> p g c u", g=PASSES, u=2),
+            )
+
+        def transposes(step):
+            k_ok, v_ok = valid(step + K_AHEAD), valid(step + V_AHEAD)
+            if not (k_ok or v_ok):
+                return
+            grouped = triple.tile([P, 2 * TOK], BF16, name="grouped", align_bytes=64)
+            kept["grouped", step] = grouped
+            if k_ok:
+                flipped_k = transpose_row("k", *divmod(step + K_AHEAD, ROWS))
+            if v_ok:
+                flipped_v = transpose_row("v", *divmod(step + V_AHEAD, ROWS))
+            if k_ok:
+                group_row(flipped_k, grouped, 0)
+            if v_ok:
+                group_row(flipped_v, grouped, 1)
+
+        def quantise_rows(step):
+            k_ok, v_ok = valid(step + K_AHEAD), valid(step + V_AHEAD)
+            if not (k_ok or v_ok):
+                return
+            codes = codes_pool.tile([P, BANK], U32, name="codes", align_bytes=64)
+            scales = codes_pool.tile([P, BANK], U8, name="scales", align_bytes=64)
+            lo = 0 if k_ok else BANK // 2
+            hi = BANK if v_ok else BANK // 2
+            nc.vector.quantize_mx(
+                out=codes[:, lo:hi].bitcast(FP8X4),
+                scales=scales[:, lo:hi],
+                in_=kept["grouped", step][:, lo * PACK : hi * PACK],
+            )
+            if k_ok:
+                kept["k_codes", step + K_AHEAD] = (codes, scales)
+            if v_ok:
+                kept["v_codes", step + V_AHEAD] = (codes, scales)
+
+        def sum_k(h, t):
+            grouped = kept["grouped", ROWS * h + t - K_AHEAD]
+            for i in range(PASSES * PACK):
+                first = (i // PACK) * P * PACK + i % PACK
+                nc.tensor.matmul(
+                    out=ksum_ps(h)[:, t : t + 1],
+                    lhsT=grouped[:, first : first + P * PACK - PACK + 1 : PACK],
+                    rhs=ones[:],
+                    start=(i == 0),
+                    stop=(i == PASSES * PACK - 1),
+                )
 
         def split_ksum(h):
-            ksum = kept["ksum", h]
+            ksum = double.tile([P, ROWS], F32, name="ksum")
             pieces = double.tile([P, ROWS, PIECES], BF16, name="ksum_pieces")
             rest1 = double.tile([P, ROWS], F32, name="rest1")
             rest2 = double.tile([P, ROWS], F32, name="rest2")
+            nc.scalar.copy(out=ksum[:], in_=ksum_ps(h))
             nc.gpsimd.tensor_copy(out=pieces[:, :, 0], in_=ksum[:])
             nc.gpsimd.tensor_tensor(out=rest1[:], in0=ksum[:], in1=pieces[:, :, 0], op=ALU.subtract)
             nc.gpsimd.tensor_copy(out=pieces[:, :, 1], in_=rest1[:])
@@ -77,70 +160,34 @@ def tile_relu_linear_att_pa_kernel(tc, q, k, v, out):
             nc.gpsimd.tensor_copy(out=pieces[:, :, 2], in_=rest2[:])
             kept["ksum_pieces", h] = pieces
 
-        def transpose_rows(h, run):
-            name = "k" if run % 2 == 0 else "v"
-            pair = run // 2
-            words = kept[name, h][:].bitcast(F32)
-            grouped = triple.tile([P, PASSES * 2 * P * PACK], BF16, name="grouped", align_bytes=64)
-            grouped_words = grouped[:].bitcast(F32)
-            for g in range(PASSES):
-                flipped = psum.tile([P, BANK], F32, name="flipped", tag="bank")
-                for b in range(2):
-                    for u in range(2):
-                        first = (2 * pair + b) * (TOK // 2) + (2 * g + u) * P
-                        block = (2 * b + u) * P
-                        nc.tensor.transpose(flipped[:, block : block + P], words[:, first : first + P], identity[:])
-                nc.scalar.copy(
-                    out=grouped_words[:, g * BANK : (g + 1) * BANK].rearrange("p (b c u) -> p b c u", b=2, u=2),
-                    in_=flipped[:].rearrange("p (b u c) -> p b c u", b=2, u=2),
-                )
-            kept["grouped", h, run] = grouped
-
-        def quantise_rows(h, run):
-            name = "k" if run % 2 == 0 else "v"
-            pair = run // 2
-            if pair == 0:
-                kept["codes", name, h] = double.tile([P, PASSES * FEAT], U32, name="codes_" + name, align_bytes=64)
-                kept["scales", name, h] = double.tile([P, PASSES * FEAT], U8, name="scales_" + name, align_bytes=64)
-            width = PASSES * 2 * P
-            nc.vector.quantize_mx(
-                out=kept["codes", name, h][:, pair * width : (pair + 1) * width].bitcast(FP8X4),
-                scales=kept["scales", name, h][:, pair * width : (pair + 1) * width],
-                in_=kept["grouped", h, run][:],
+        def group_q(h, j):
+            if j == 0:
+                kept["q_grouped", h] = double.tile([P, TOK * PACK], BF16, name="q_grouped", align_bytes=64)
+            dst = kept["q_grouped", h][:, j * Q_CHUNK * PACK : (j + 1) * Q_CHUNK * PACK].rearrange(
+                "p (c i t) -> p c t i", i=4, t=PACK
             )
-
-        def row_block(t, g):
-            first = (((t // 2) * PASSES + g) * 2 + t % 2) * P
-            return slice(first, first + P)
-
-        def prepare_q(h, part):
-            q_rows = kept["q", h]
-            if part == 0:
-                nc.vector.tensor_scalar_max(out=q_rows[:], in0=q_rows[:], scalar1=0.0)
-                kept["q_grouped", h] = single.tile([P, TOK * PACK], BF16, name="q_grouped", align_bytes=64)
-            elif part <= HALVES:
-                half = part - 1
-                nc.vector.tensor_copy(
-                    out=kept["q_grouped", h][:, half * BANK * PACK : (half + 1) * BANK * PACK].rearrange(
-                        "p (c i t) -> p c t i", i=4, t=PACK
-                    ),
-                    in_=q_rows[:].rearrange("p (t n) -> p t n", t=ROWS)[:, :, half * BANK : (half + 1) * BANK].rearrange(
-                        "p t (c i) -> p c t i", i=4
-                    ),
-                )
+            source = kept["q", h][:].rearrange("p (t n) -> p t n", t=ROWS)[:, :, j * Q_CHUNK : (j + 1) * Q_CHUNK].rearrange(
+                "p t (c i) -> p c t i", i=4
+            )
+            if j in S_CHUNKS[h]:
+                nc.scalar.activation(out=dst, in_=source, func=ACT.Relu)
             else:
-                kept["q_codes", h] = triple.tile([P, TOK], U32, name="q_codes", align_bytes=64)
-                kept["q_scales", h] = triple.tile([P, TOK], U8, name="q_scales", align_bytes=64)
-                nc.vector.quantize_mx(
-                    out=kept["q_codes", h][:].bitcast(FP8X4), scales=kept["q_scales", h][:], in_=kept["q_grouped", h][:]
-                )
+                nc.vector.tensor_scalar_max(out=dst, in0=source, scalar1=0.0)
+
+        def quantise_q(h):
+            kept["q_codes", h] = double.tile([P, TOK], U32, name="q_codes", align_bytes=64)
+            kept["q_scales", h] = double.tile([P, TOK], U8, name="q_scales", align_bytes=64)
+            nc.vector.quantize_mx(
+                out=kept["q_codes", h][:].bitcast(FP8X4), scales=kept["q_scales", h][:], in_=kept["q_grouped", h][:]
+            )
 
         def den_matmuls(h, tiles):
             for j in tiles:
                 for t in range(ROWS):
+                    first = j * P * PACK + t
                     nc.tensor.matmul(
-                        out=kept["den_ps", h][:, j, :],
-                        lhsT=kept["q", h][:, t * TOK + j * P : t * TOK + (j + 1) * P],
+                        out=den_ps(h)[:, j, :],
+                        lhsT=kept["q_grouped", h][:, first : first + P * PACK - PACK + 1 : PACK],
                         rhs=kept["ksum_pieces", h][:, t, :],
                         start=(t == 0),
                         stop=(t == ROWS - 1),
@@ -149,7 +196,7 @@ def tile_relu_linear_att_pa_kernel(tc, q, k, v, out):
         def reciprocal_den(h):
             den = double.tile([P, TOK_TILES], F32, name="den")
             rden = double.tile([P, TOK_TILES], F32, name="rden")
-            nc.vector.tensor_reduce(out=den[:], in_=kept["den_ps", h][:], axis=mybir.AxisListType.X, op=ALU.add)
+            nc.vector.tensor_reduce(out=den[:], in_=den_ps(h), axis=mybir.AxisListType.X, op=ALU.add)
             nc.vector.reciprocal(out=rden[:], in_=den[:])
             kept["rden", h] = rden
 
@@ -166,14 +213,18 @@ def tile_relu_linear_att_pa_kernel(tc, q, k, v, out):
 
         def first_matmul(h, c):
             vk_ps = psum.tile([P, BANK], F32, name="vk_ps", tag="bank")
+            v_codes, v_scales = kept["v_codes", ROWS * h + c]
             for t in range(ROWS):
+                k_codes, k_scales = kept["k_codes", ROWS * h + t]
                 for g in range(PASSES):
+                    k_cols = slice(g * P, (g + 1) * P)
+                    v_cols = slice(BANK // 2 + g * P, BANK // 2 + (g + 1) * P)
                     nc.tensor.matmul_mx(
                         out=vk_ps[:, t * P : (t + 1) * P],
-                        lhsT=kept["codes", "k", h][:, row_block(t, g)].bitcast(FP8X4),
-                        lhsT_scale=kept["scales", "k", h][:, row_block(t, g)],
-                        rhs=kept["codes", "v", h][:, row_block(c, g)].bitcast(FP8X4),
-                        rhs_scale=kept["scales", "v", h][:, row_block(c, g)],
+                        lhsT=k_codes[:, k_cols].bitcast(FP8X4),
+                        lhsT_scale=k_scales[:, k_cols],
+                        rhs=v_codes[:, v_cols].bitcast(FP8X4),
+                        rhs_scale=v_scales[:, v_cols],
                         start=(g == 0),
                         stop=(g == PASSES - 1),
                     )
@@ -220,46 +271,46 @@ def tile_relu_linear_att_pa_kernel(tc, q, k, v, out):
                 )
                 nc.sync.dma_start(out=out_view[:, c, h // 2, h % 2, n_cols], in_=result[:])
 
-        for t in range(ROWS):
-            load("k", k, 0, t, 1)
-        load("v", v, 0, 0, ROWS // 2)
-        load("q", q, 0, 0, ROWS)
-        load("v", v, 0, ROWS // 2, ROWS // 2)
-        for h in range(1, HEADS):
-            load("k", k, h, 0, ROWS)
-            load("q", q, h, 0, ROWS)
-            load("v", v, h, 0, ROWS)
+        every = slice(0, ROWS)
+        all_tok = slice(0, TOK)
+        src = {"k": k, "q": q, "v": v}
+        for item in LOADS.split():
+            nm = item[0]
+            hd = int(item[1])
+            rows = slice(int(item[2]), int(item[-1]) + 1) if len(item) > 2 else every
+            load(nm, src[nm], hd, rows, all_tok)
 
         def valid(quarter):
             return 0 <= quarter < QUARTERS
 
-        for step in range(-EARLY, QUARTERS + BEHIND):
-            if valid(step) and step % ROWS == 1:
-                reciprocal_den(step // ROWS)
-            if valid(step + AHEAD):
-                transpose_rows(*divmod(step + AHEAD, ROWS))
-            if valid(step + AHEAD - 1):
-                quantise_rows(*divmod(step + AHEAD - 1, ROWS))
+        for step in range(-RELU_AHEAD, QUARTERS + BEHIND):
+            head, c = divmod(step, ROWS)
+            if valid(step + RELU_AHEAD) and not RELU_LATE:
+                relu_k(*divmod(step + RELU_AHEAD, ROWS))
+            transposes(step)
+            quantise_rows(step - 1)
             if valid(step - BEHIND):
                 second_matmul(*divmod(step - BEHIND, ROWS))
             if valid(step - 1):
                 quantise_vk(*divmod(step - 1, ROWS))
-            if valid(step + EARLY):
-                relu_k(*divmod(step + EARLY, ROWS))
-                if (step + EARLY) % ROWS == ROWS - 1:
-                    split_ksum((step + EARLY) // ROWS)
+            if valid(step + Q_AHEAD):
+                group_q(*divmod(step + Q_AHEAD, ROWS))
             if valid(step):
-                first_matmul(*divmod(step, ROWS))
-            if valid(step + EARLY):
-                prepare_q(*divmod(step + EARLY, ROWS))
-            if valid(step):
-                round_vk(*divmod(step, ROWS))
-            if valid(step) and step % ROWS == 1:
-                spread_rden(step // ROWS)
-            if valid(step + 1) and (step + 1) % ROWS == 0:
-                kept["den_ps", (step + 1) // ROWS] = psum_den.tile([P, TOK_TILES, PIECES], F32, name="den_ps")
-                den_matmuls((step + 1) // ROWS, range(0, TOK_TILES // 2))
-            if valid(step) and step % ROWS == 0:
-                den_matmuls(step // ROWS, range(TOK_TILES // 2, TOK_TILES))
+                first_matmul(head, c)
+                round_vk(head, c)
+            if valid(step + KSUM_AHEAD):
+                sum_k(*divmod(step + KSUM_AHEAD, ROWS))
+                if (step + KSUM_AHEAD) % ROWS == ROWS - 1:
+                    split_ksum((step + KSUM_AHEAD) // ROWS)
+            if valid(step - QQ_STEP) and (step - QQ_STEP) % ROWS == 0:
+                quantise_q((step - QQ_STEP) // ROWS)
+            for i in range(2):
+                if valid(step - DEN_STEPS[i]) and (step - DEN_STEPS[i]) % ROWS == 0:
+                    den_matmuls((step - DEN_STEPS[i]) // ROWS, range(i * TOK_TILES // 2, (i + 1) * TOK_TILES // 2))
             if valid(step - BEHIND):
                 divide_and_store(*divmod(step - BEHIND, ROWS))
+            if valid(step + RELU_AHEAD) and RELU_LATE:
+                relu_k(*divmod(step + RELU_AHEAD, ROWS))
+            if valid(step - RDEN_STEP) and (step - RDEN_STEP) % ROWS == 0:
+                reciprocal_den((step - RDEN_STEP) // ROWS)
+                spread_rden((step - RDEN_STEP) // ROWS)

@@ -29,14 +29,15 @@ RELU_AHEAD = 7
 K_AHEAD = 6
 KSUM_AHEAD = 5
 Q_AHEAD = 4
-V_AHEAD = 3
-BEHIND = 2
+V_AHEAD = 4
+BEHIND = 3
 DEN_STEPS = (0, 0)
 RDEN_STEP = 0
-QQ_STEP = 1
-S_CHUNKS = ((0, 2), (0, 2), (0, 2), (0, 2))
-RELU_LATE = False
-K_LATE = 0
+QQ_STEP = -1
+Q_ENG = ("VGSG", "GGGG", "GGGG", "GGGG")
+ROW_ENG = "VVVS"
+BIG = 3.3895313892515355e38
+ORDER = "GDRXMVKFUCTQYS"
 LOADS = "k00 k01 k02 k03 q0 v001 k101 v023 k123 q1 v101 k201 v123 k223 q2 v2 k3 q3 v3"
 QUARTERS = HEADS * ROWS
 
@@ -83,8 +84,17 @@ def tile_relu_linear_att_pa_kernel(tc, q, k, v, out):
             return small[:, first : first + TOK_TILES * PIECES].rearrange("p (j i) -> p j i", i=PIECES)
 
         def relu_k(h, t):
+            if t == 0:
+                kept["ksum", h] = double.tile([P, ROWS], F32, name="ksum")
             row = kept["k", h][:, t * TOK : (t + 1) * TOK]
-            nc.vector.tensor_scalar_max(out=row, in0=row, scalar1=0.0)
+            if ROW_ENG[t] == "S":
+                nc.scalar.activation(out=row, in_=row, func=ACT.Relu, accum_out=kept["ksum", h][:, t : t + 1])
+            elif ROW_ENG[t] == "V":
+                nc.vector.tensor_scalar(
+                    out=row, in0=row, scalar1=0.0, scalar2=None, op0=ALU.max, op1=ALU.add, accum_out=kept["ksum", h][:, t : t + 1]
+                )
+            else:
+                nc.vector.tensor_scalar_max(out=row, in0=row, scalar1=0.0)
 
         def transpose_row(name, h, t):
             words = kept[name, h][:].bitcast(F32)
@@ -136,6 +146,8 @@ def tile_relu_linear_att_pa_kernel(tc, q, k, v, out):
                 kept["v_codes", step + V_AHEAD] = (codes, scales)
 
         def sum_k(h, t):
+            if ROW_ENG[t] != "P":
+                return
             grouped = kept["grouped", ROWS * h + t - K_AHEAD]
             for i in range(PASSES * PACK):
                 first = (i // PACK) * P * PACK + i % PACK
@@ -148,11 +160,13 @@ def tile_relu_linear_att_pa_kernel(tc, q, k, v, out):
                 )
 
         def split_ksum(h):
-            ksum = double.tile([P, ROWS], F32, name="ksum")
+            ksum = kept["ksum", h]
+            n_pe = ROW_ENG.count("P")
             pieces = double.tile([P, ROWS, PIECES], BF16, name="ksum_pieces")
             rest1 = double.tile([P, ROWS], F32, name="rest1")
             rest2 = double.tile([P, ROWS], F32, name="rest2")
-            nc.scalar.copy(out=ksum[:], in_=ksum_ps(h))
+            if n_pe:
+                nc.scalar.copy(out=ksum[:, :n_pe], in_=ksum_ps(h)[:, :n_pe])
             nc.gpsimd.tensor_copy(out=pieces[:, :, 0], in_=ksum[:])
             nc.gpsimd.tensor_tensor(out=rest1[:], in0=ksum[:], in1=pieces[:, :, 0], op=ALU.subtract)
             nc.gpsimd.tensor_copy(out=pieces[:, :, 1], in_=rest1[:])
@@ -169,8 +183,10 @@ def tile_relu_linear_att_pa_kernel(tc, q, k, v, out):
             source = kept["q", h][:].rearrange("p (t n) -> p t n", t=ROWS)[:, :, j * Q_CHUNK : (j + 1) * Q_CHUNK].rearrange(
                 "p t (c i) -> p c t i", i=4
             )
-            if j in S_CHUNKS[h]:
+            if Q_ENG[h][j] == "S":
                 nc.scalar.activation(out=dst, in_=source, func=ACT.Relu)
+            elif Q_ENG[h][j] == "G":
+                nc.gpsimd.tensor_scalar(out=dst, in0=source, scalar1=BIG, scalar2=0.0, op0=ALU.min, op1=ALU.max)
             else:
                 nc.vector.tensor_scalar_max(out=dst, in0=source, scalar1=0.0)
 
@@ -284,33 +300,36 @@ def tile_relu_linear_att_pa_kernel(tc, q, k, v, out):
             return 0 <= quarter < QUARTERS
 
         for step in range(-RELU_AHEAD, QUARTERS + BEHIND):
-            head, c = divmod(step, ROWS)
-            if valid(step + RELU_AHEAD) and not RELU_LATE:
-                relu_k(*divmod(step + RELU_AHEAD, ROWS))
-            transposes(step)
-            quantise_rows(step - 1)
-            if valid(step - BEHIND):
-                second_matmul(*divmod(step - BEHIND, ROWS))
-            if valid(step - 1):
-                quantise_vk(*divmod(step - 1, ROWS))
-            if valid(step + Q_AHEAD):
-                group_q(*divmod(step + Q_AHEAD, ROWS))
-            if valid(step):
-                first_matmul(head, c)
-                round_vk(head, c)
-            if valid(step + KSUM_AHEAD):
-                sum_k(*divmod(step + KSUM_AHEAD, ROWS))
-                if (step + KSUM_AHEAD) % ROWS == ROWS - 1:
-                    split_ksum((step + KSUM_AHEAD) // ROWS)
-            if valid(step - QQ_STEP) and (step - QQ_STEP) % ROWS == 0:
-                quantise_q((step - QQ_STEP) // ROWS)
-            for i in range(2):
-                if valid(step - DEN_STEPS[i]) and (step - DEN_STEPS[i]) % ROWS == 0:
-                    den_matmuls((step - DEN_STEPS[i]) // ROWS, range(i * TOK_TILES // 2, (i + 1) * TOK_TILES // 2))
-            if valid(step - BEHIND):
-                divide_and_store(*divmod(step - BEHIND, ROWS))
-            if valid(step + RELU_AHEAD) and RELU_LATE:
-                relu_k(*divmod(step + RELU_AHEAD, ROWS))
-            if valid(step - RDEN_STEP) and (step - RDEN_STEP) % ROWS == 0:
-                reciprocal_den((step - RDEN_STEP) // ROWS)
-                spread_rden((step - RDEN_STEP) // ROWS)
+            for stage in ORDER:
+                if stage == "R" and valid(step + RELU_AHEAD):
+                    relu_k(*divmod(step + RELU_AHEAD, ROWS))
+                if stage == "T":
+                    transposes(step)
+                if stage == "K":
+                    quantise_rows(step - 1)
+                if stage == "M" and valid(step - BEHIND):
+                    second_matmul(*divmod(step - BEHIND, ROWS))
+                if stage == "U" and valid(step - 1):
+                    quantise_vk(*divmod(step - 1, ROWS))
+                if stage == "G" and valid(step + Q_AHEAD):
+                    group_q(*divmod(step + Q_AHEAD, ROWS))
+                if stage == "F" and valid(step):
+                    first_matmul(*divmod(step, ROWS))
+                if stage == "C" and valid(step):
+                    round_vk(*divmod(step, ROWS))
+                if stage == "S" and valid(step + KSUM_AHEAD):
+                    sum_k(*divmod(step + KSUM_AHEAD, ROWS))
+                    if (step + KSUM_AHEAD) % ROWS == ROWS - 1:
+                        split_ksum((step + KSUM_AHEAD) // ROWS)
+                if stage == "Q" and valid(step - QQ_STEP) and (step - QQ_STEP) % ROWS == 0:
+                    quantise_q((step - QQ_STEP) // ROWS)
+                if stage == "D":
+                    for i in range(2):
+                        if valid(step - DEN_STEPS[i]) and (step - DEN_STEPS[i]) % ROWS == 0:
+                            den_matmuls((step - DEN_STEPS[i]) // ROWS, range(i * TOK_TILES // 2, (i + 1) * TOK_TILES // 2))
+                if stage == "V" and valid(step - BEHIND):
+                    divide_and_store(*divmod(step - BEHIND, ROWS))
+                if stage == "X" and valid(step - RDEN_STEP) and (step - RDEN_STEP) % ROWS == 0:
+                    reciprocal_den((step - RDEN_STEP) // ROWS)
+                if stage == "Y" and valid(step - RDEN_STEP) and (step - RDEN_STEP) % ROWS == 0:
+                    spread_rden((step - RDEN_STEP) // ROWS)

@@ -31,14 +31,16 @@ KSUM_AHEAD = 5
 Q_AHEAD = 4
 V_AHEAD = 4
 BEHIND = 3
-DEN_STEPS = (0, 0)
-RDEN_STEP = 0
-QQ_STEP = -1
-Q_ENG = ("VGSG", "GGGG", "GGGG", "GGGG")
+DEN_STEPS = (-1, 0)
+RDEN_STEP = 1
+QQ_STEP = 0
+Q_ENG = ("VVSV", "GVGS", "GVGS", "GVGS")
 ROW_ENG = "VVVS"
+ROW0_ENG = "VVVV"
+PAIR_FROM = 99
 BIG = 3.3895313892515355e38
-ORDER = "GDRXMVKFUCTQYS"
-LOADS = "k00 k01 k02 k03 q0 v001 k101 v023 k123 q1 v101 k201 v123 k223 q2 v2 k3 q3 v3"
+ORDER = "ZXMFVCKURDQSGTY"
+LOADS = "k00 k01 k02 k03 v001 q0 k101 v023 k123 q1 v101 k201 v123 k223 q2 v2 k3 q3 v3"
 QUARTERS = HEADS * ROWS
 
 FLOPS = 2 * 2 * HEADS * FEAT * FEAT * TOK
@@ -53,6 +55,7 @@ def tile_relu_linear_att_pa_kernel(tc, q, k, v, out):
         inputs = ctx.enter_context(tc.tile_pool(name="inputs", bufs=HEADS))
         double = ctx.enter_context(tc.tile_pool(name="double", bufs=2))
         triple = ctx.enter_context(tc.tile_pool(name="triple", bufs=3))
+        quad = ctx.enter_context(tc.tile_pool(name="quad", bufs=4))
         codes_pool = ctx.enter_context(tc.tile_pool(name="codes_pool", bufs=11))
         results = ctx.enter_context(tc.tile_pool(name="results", bufs=6))
         psum = ctx.enter_context(tc.psum_pool(name="psum", bufs=7))
@@ -75,6 +78,9 @@ def tile_relu_linear_att_pa_kernel(tc, q, k, v, out):
                 in_=src[0, h].rearrange("(p t) n -> p t n", t=ROWS)[:, rows, cols],
             )
 
+        def rows_of(h):
+            return ROW_ENG if h else ROW0_ENG
+
         def ksum_ps(h):
             first = (h % 2) * SMALL
             return small[:, first : first + ROWS]
@@ -87,9 +93,9 @@ def tile_relu_linear_att_pa_kernel(tc, q, k, v, out):
             if t == 0:
                 kept["ksum", h] = double.tile([P, ROWS], F32, name="ksum")
             row = kept["k", h][:, t * TOK : (t + 1) * TOK]
-            if ROW_ENG[t] == "S":
+            if rows_of(h)[t] == "S":
                 nc.scalar.activation(out=row, in_=row, func=ACT.Relu, accum_out=kept["ksum", h][:, t : t + 1])
-            elif ROW_ENG[t] == "V":
+            elif rows_of(h)[t] == "V":
                 nc.vector.tensor_scalar(
                     out=row, in0=row, scalar1=0.0, scalar2=None, op0=ALU.max, op1=ALU.add, accum_out=kept["ksum", h][:, t : t + 1]
                 )
@@ -116,7 +122,7 @@ def tile_relu_linear_att_pa_kernel(tc, q, k, v, out):
             k_ok, v_ok = valid(step + K_AHEAD), valid(step + V_AHEAD)
             if not (k_ok or v_ok):
                 return
-            grouped = triple.tile([P, 2 * TOK], BF16, name="grouped", align_bytes=64)
+            grouped = quad.tile([P, 2 * TOK], BF16, name="grouped", align_bytes=64)
             kept["grouped", step] = grouped
             if k_ok:
                 flipped_k = transpose_row("k", *divmod(step + K_AHEAD, ROWS))
@@ -146,7 +152,7 @@ def tile_relu_linear_att_pa_kernel(tc, q, k, v, out):
                 kept["v_codes", step + V_AHEAD] = (codes, scales)
 
         def sum_k(h, t):
-            if ROW_ENG[t] != "P":
+            if rows_of(h)[t] != "P":
                 return
             grouped = kept["grouped", ROWS * h + t - K_AHEAD]
             for i in range(PASSES * PACK):
@@ -161,7 +167,7 @@ def tile_relu_linear_att_pa_kernel(tc, q, k, v, out):
 
         def split_ksum(h):
             ksum = kept["ksum", h]
-            n_pe = ROW_ENG.count("P")
+            n_pe = rows_of(h).count("P")
             pieces = double.tile([P, ROWS, PIECES], BF16, name="ksum_pieces")
             rest1 = double.tile([P, ROWS], F32, name="rest1")
             rest2 = double.tile([P, ROWS], F32, name="rest2")
@@ -210,11 +216,14 @@ def tile_relu_linear_att_pa_kernel(tc, q, k, v, out):
                     )
 
         def reciprocal_den(h):
-            den = double.tile([P, TOK_TILES], F32, name="den")
             rden = double.tile([P, TOK_TILES], F32, name="rden")
-            nc.vector.tensor_reduce(out=den[:], in_=den_ps(h), axis=mybir.AxisListType.X, op=ALU.add)
-            nc.vector.reciprocal(out=rden[:], in_=den[:])
+            nc.vector.reciprocal(out=rden[:], in_=kept["den", h][:])
             kept["rden", h] = rden
+
+        def reduce_den(h):
+            den = double.tile([P, TOK_TILES], F32, name="den")
+            nc.vector.tensor_reduce(out=den[:], in_=den_ps(h), axis=mybir.AxisListType.X, op=ALU.add)
+            kept["den", h] = den
 
         def spread_rden(h):
             kept["rden_rows", h] = double.tile([P, TOK], F32, name="rden_rows")
@@ -304,7 +313,11 @@ def tile_relu_linear_att_pa_kernel(tc, q, k, v, out):
                 if stage == "R" and valid(step + RELU_AHEAD):
                     relu_k(*divmod(step + RELU_AHEAD, ROWS))
                 if stage == "T":
-                    transposes(step)
+                    if step < PAIR_FROM:
+                        transposes(step)
+                    elif step % 2 == 0:
+                        transposes(step)
+                        transposes(step + 1)
                 if stage == "K":
                     quantise_rows(step - 1)
                 if stage == "M" and valid(step - BEHIND):
@@ -329,6 +342,8 @@ def tile_relu_linear_att_pa_kernel(tc, q, k, v, out):
                             den_matmuls((step - DEN_STEPS[i]) // ROWS, range(i * TOK_TILES // 2, (i + 1) * TOK_TILES // 2))
                 if stage == "V" and valid(step - BEHIND):
                     divide_and_store(*divmod(step - BEHIND, ROWS))
+                if stage == "Z" and valid(step - RDEN_STEP) and (step - RDEN_STEP) % ROWS == 0:
+                    reduce_den((step - RDEN_STEP) // ROWS)
                 if stage == "X" and valid(step - RDEN_STEP) and (step - RDEN_STEP) % ROWS == 0:
                     reciprocal_den((step - RDEN_STEP) // ROWS)
                 if stage == "Y" and valid(step - RDEN_STEP) and (step - RDEN_STEP) % ROWS == 0:

@@ -25,22 +25,25 @@ PIECES = 3
 SMALL = ROWS + TOK_TILES * PIECES
 Q_CHUNK = TOK // ROWS
 
-RELU_AHEAD = 7
+RELU_AHEAD = 8
 K_AHEAD = 6
 KSUM_AHEAD = 5
 Q_AHEAD = 4
-V_AHEAD = 4
+V_AHEAD = 2
 BEHIND = 3
 DEN_STEPS = (-1, 0)
 RDEN_STEP = 1
 QQ_STEP = 0
-Q_ENG = ("VVSV", "GVGS", "GVGS", "GVGS")
-ROW_ENG = "VVVS"
-ROW0_ENG = "VVVV"
-PAIR_FROM = 99
+Q_ENG = ('VVGV', 'GVGG', 'GVGG', 'SSVG')
+ROW_ENG = 'VSVS'
+ROW0_ENG = 'VVVV'
+PAIR_FROM = 0
+G_PIECES = 1
 BIG = 3.3895313892515355e38
-ORDER = "ZXMFVCKURDQSGTY"
-LOADS = "k00 k01 k02 k03 v001 q0 k101 v023 k123 q1 v101 k201 v123 k223 q2 v2 k3 q3 v3"
+ORDER = 'ZXMVKQUSRGTDFCY'
+DMA_FROM = 9
+LOADS2 = ''
+LOADS = 'k00 k01 k02 k03 k101 q0 v001 k123 v023 q1 k201 v101 k223 v123 q2 v2 k3 v3 q3'
 QUARTERS = HEADS * ROWS
 
 FLOPS = 2 * 2 * HEADS * FEAT * FEAT * TOK
@@ -56,8 +59,9 @@ def tile_relu_linear_att_pa_kernel(tc, q, k, v, out):
         double = ctx.enter_context(tc.tile_pool(name="double", bufs=2))
         triple = ctx.enter_context(tc.tile_pool(name="triple", bufs=3))
         quad = ctx.enter_context(tc.tile_pool(name="quad", bufs=4))
-        codes_pool = ctx.enter_context(tc.tile_pool(name="codes_pool", bufs=11))
-        results = ctx.enter_context(tc.tile_pool(name="results", bufs=6))
+        vk_pool = ctx.enter_context(tc.tile_pool(name="vk_pool", bufs=6))
+        codes_pool = ctx.enter_context(tc.tile_pool(name="codes_pool", bufs=15))
+        results = ctx.enter_context(tc.tile_pool(name="results", bufs=10))
         psum = ctx.enter_context(tc.psum_pool(name="psum", bufs=7))
         psum_small = ctx.enter_context(tc.psum_pool(name="psum_small", bufs=1))
         ctx.enter_context(tc.manual_schedule())
@@ -183,22 +187,26 @@ def tile_relu_linear_att_pa_kernel(tc, q, k, v, out):
         def group_q(h, j):
             if j == 0:
                 kept["q_grouped", h] = double.tile([P, TOK * PACK], BF16, name="q_grouped", align_bytes=64)
-            dst = kept["q_grouped", h][:, j * Q_CHUNK * PACK : (j + 1) * Q_CHUNK * PACK].rearrange(
-                "p (c i t) -> p c t i", i=4, t=PACK
-            )
-            source = kept["q", h][:].rearrange("p (t n) -> p t n", t=ROWS)[:, :, j * Q_CHUNK : (j + 1) * Q_CHUNK].rearrange(
+            n_pieces = G_PIECES if Q_ENG[h][j] == "G" else 1
+            width = Q_CHUNK // n_pieces
+            for i in range(n_pieces):
+                group_tokens(h, Q_ENG[h][j], j * Q_CHUNK + i * width, width)
+
+        def group_tokens(h, engine, first, width):
+            dst = kept["q_grouped", h][:, first * PACK : (first + width) * PACK].rearrange("p (c i t) -> p c t i", i=4, t=PACK)
+            source = kept["q", h][:].rearrange("p (t n) -> p t n", t=ROWS)[:, :, first : first + width].rearrange(
                 "p t (c i) -> p c t i", i=4
             )
-            if Q_ENG[h][j] == "S":
+            if engine == "S":
                 nc.scalar.activation(out=dst, in_=source, func=ACT.Relu)
-            elif Q_ENG[h][j] == "G":
+            elif engine == "G":
                 nc.gpsimd.tensor_scalar(out=dst, in0=source, scalar1=BIG, scalar2=0.0, op0=ALU.min, op1=ALU.max)
             else:
                 nc.vector.tensor_scalar_max(out=dst, in0=source, scalar1=0.0)
 
         def quantise_q(h):
-            kept["q_codes", h] = double.tile([P, TOK], U32, name="q_codes", align_bytes=64)
-            kept["q_scales", h] = double.tile([P, TOK], U8, name="q_scales", align_bytes=64)
+            kept["q_codes", h] = triple.tile([P, TOK], U32, name="q_codes", align_bytes=64)
+            kept["q_scales", h] = triple.tile([P, TOK], U8, name="q_scales", align_bytes=64)
             nc.vector.quantize_mx(
                 out=kept["q_codes", h][:].bitcast(FP8X4), scales=kept["q_scales", h][:], in_=kept["q_grouped", h][:]
             )
@@ -206,10 +214,11 @@ def tile_relu_linear_att_pa_kernel(tc, q, k, v, out):
         def den_matmuls(h, tiles):
             for j in tiles:
                 for t in range(ROWS):
-                    first = j * P * PACK + t
+                    first = (j * PACK if h >= DMA_FROM else j * P * PACK) + t
+                    apart = TOK_TILES * PACK if h >= DMA_FROM else PACK
                     nc.tensor.matmul(
                         out=den_ps(h)[:, j, :],
-                        lhsT=kept["q_grouped", h][:, first : first + P * PACK - PACK + 1 : PACK],
+                        lhsT=kept["q_grouped", h][:, first : first + (P - 1) * apart + 1 : apart],
                         rhs=kept["ksum_pieces", h][:, t, :],
                         start=(t == 0),
                         stop=(t == ROWS - 1),
@@ -226,7 +235,14 @@ def tile_relu_linear_att_pa_kernel(tc, q, k, v, out):
             kept["den", h] = den
 
         def spread_rden(h):
-            kept["rden_rows", h] = double.tile([P, TOK], F32, name="rden_rows")
+            kept["rden_rows", h] = triple.tile([P, TOK], F32, name="rden_rows")
+            if h >= DMA_FROM:
+                row = out[0, (FEAT - 1) * 2 + h // 2, (h % 2) * TOK : (h % 2 + 1) * TOK]
+                nc.sync.dma_start(out=row.rearrange("(p j) -> p j", j=TOK_TILES), in_=kept["rden", h][:])
+                nc.sync.dma_start(out=kept["rden_rows", h][:], in_=row.partition_broadcast(P))
+                if h == DMA_FROM:
+                    load_list(LOADS2)
+                return
             for half in range(HALVES):
                 spread = psum.tile([P, BANK], F32, name="spread", tag="bank")
                 for jj in range(BANK // P):
@@ -264,8 +280,8 @@ def tile_relu_linear_att_pa_kernel(tc, q, k, v, out):
             kept["vk_grouped", h, c] = vk_grouped
 
         def quantise_vk(h, c):
-            kept["vk_codes", h, c] = triple.tile([P, P], U32, name="vk_codes", align_bytes=64)
-            kept["vk_scales", h, c] = triple.tile([P, P], U8, name="vk_scales", align_bytes=64)
+            kept["vk_codes", h, c] = vk_pool.tile([P, P], U32, name="vk_codes", align_bytes=64)
+            kept["vk_scales", h, c] = vk_pool.tile([P, P], U8, name="vk_scales", align_bytes=64)
             nc.vector.quantize_mx(
                 out=kept["vk_codes", h, c][:].bitcast(FP8X4),
                 scales=kept["vk_scales", h, c][:],
@@ -299,11 +315,15 @@ def tile_relu_linear_att_pa_kernel(tc, q, k, v, out):
         every = slice(0, ROWS)
         all_tok = slice(0, TOK)
         src = {"k": k, "q": q, "v": v}
-        for item in LOADS.split():
-            nm = item[0]
-            hd = int(item[1])
-            rows = slice(int(item[2]), int(item[-1]) + 1) if len(item) > 2 else every
-            load(nm, src[nm], hd, rows, all_tok)
+
+        def load_list(items):
+            for item in items.split():
+                nm = item[0]
+                hd = int(item[1])
+                rows = slice(int(item[2]), int(item[-1]) + 1) if len(item) > 2 else every
+                load(nm, src[nm], hd, rows, all_tok)
+
+        load_list(LOADS)
 
         def valid(quarter):
             return 0 <= quarter < QUARTERS

@@ -22,31 +22,21 @@ BANK = 512
 HALVES = TOK // BANK
 TOK_TILES = TOK // P
 PIECES = 3
-SMALL = ROWS + TOK_TILES * PIECES
-Q_CHUNK = TOK // ROWS
+CHUNK = TOK // ROWS
+LARGEST = 3.3895313892515355e38
 
 RELU_AHEAD = 8
 K_AHEAD = 6
-KSUM_AHEAD = 5
 Q_AHEAD = 4
 V_AHEAD = 2
 BEHIND = 3
-DEN_STEPS = (-1, 0)
-RDEN_STEP = 1
-QQ_STEP = 0
-Q_ENG = ('VVGV', 'GVGG', 'GVGG', 'SSVG')
-ROW_ENG = 'VSVS'
-ROW0_ENG = 'VVVV'
-PAIR_FROM = 0
-G_PIECES = 1
-BIG = 3.3895313892515355e38
-ORDER = 'ZXMVKQUSRGTDFCY'
-DMA_FROM = 9
-LOADS2 = ''
-LOADS = 'k00 k01 k02 k03 k101 q0 v001 k123 v023 q1 k201 v101 k223 v123 q2 v2 k3 v3 q3'
 QUARTERS = HEADS * ROWS
 
 FLOPS = 2 * 2 * HEADS * FEAT * FEAT * TOK
+
+ROW_ENGINE = "VVVS"
+Q_ENGINE = ("VVVV", "GVGS", "GVGS", "GSGS")
+G_PIECES = 2
 
 
 def tile_relu_linear_att_pa_kernel(tc, q, k, v, out):
@@ -59,52 +49,48 @@ def tile_relu_linear_att_pa_kernel(tc, q, k, v, out):
         double = ctx.enter_context(tc.tile_pool(name="double", bufs=2))
         triple = ctx.enter_context(tc.tile_pool(name="triple", bufs=3))
         quad = ctx.enter_context(tc.tile_pool(name="quad", bufs=4))
-        vk_pool = ctx.enter_context(tc.tile_pool(name="vk_pool", bufs=6))
-        codes_pool = ctx.enter_context(tc.tile_pool(name="codes_pool", bufs=15))
-        results = ctx.enter_context(tc.tile_pool(name="results", bufs=10))
+        row_codes = ctx.enter_context(tc.tile_pool(name="row_codes", bufs=10))
+        results = ctx.enter_context(tc.tile_pool(name="results", bufs=8))
         psum = ctx.enter_context(tc.psum_pool(name="psum", bufs=7))
-        psum_small = ctx.enter_context(tc.psum_pool(name="psum_small", bufs=1))
+        psum_den = ctx.enter_context(tc.psum_pool(name="psum_den", bufs=1))
         ctx.enter_context(tc.manual_schedule())
 
         identity = consts.tile([P, P], F32)
         make_identity(nc, identity[:])
-        ones = consts.tile([P, 1], BF16)
-        nc.gpsimd.memset(ones[:], 1.0)
-        small = psum_small.tile([P, 2 * SMALL], F32, name="small")
 
         kept = {}
 
-        def load(name, src, h, rows, cols):
+        def load(name, src, h, first_row, n_rows):
             if (name, h) not in kept:
                 kept[name, h] = inputs.tile([P, ROWS * TOK], BF16, name=name + "_rows")
+            cols = slice(first_row * TOK, (first_row + n_rows) * TOK)
             nc.sync.dma_start(
-                out=kept[name, h][:].rearrange("p (t n) -> p t n", t=ROWS)[:, rows, cols],
-                in_=src[0, h].rearrange("(p t) n -> p t n", t=ROWS)[:, rows, cols],
+                out=kept[name, h][:, cols], in_=src[0, h].rearrange("(p t) n -> p (t n)", t=ROWS)[:, cols]
             )
-
-        def rows_of(h):
-            return ROW_ENG if h else ROW0_ENG
-
-        def ksum_ps(h):
-            first = (h % 2) * SMALL
-            return small[:, first : first + ROWS]
-
-        def den_ps(h):
-            first = (h % 2) * SMALL + ROWS
-            return small[:, first : first + TOK_TILES * PIECES].rearrange("p (j i) -> p j i", i=PIECES)
 
         def relu_k(h, t):
             if t == 0:
                 kept["ksum", h] = double.tile([P, ROWS], F32, name="ksum")
             row = kept["k", h][:, t * TOK : (t + 1) * TOK]
-            if rows_of(h)[t] == "S":
-                nc.scalar.activation(out=row, in_=row, func=ACT.Relu, accum_out=kept["ksum", h][:, t : t + 1])
-            elif rows_of(h)[t] == "V":
-                nc.vector.tensor_scalar(
-                    out=row, in0=row, scalar1=0.0, scalar2=None, op0=ALU.max, op1=ALU.add, accum_out=kept["ksum", h][:, t : t + 1]
-                )
+            total = kept["ksum", h][:, t : t + 1]
+            if ROW_ENGINE[t] == "S":
+                nc.scalar.activation(out=row, in_=row, func=ACT.Relu, accum_out=total)
             else:
-                nc.vector.tensor_scalar_max(out=row, in0=row, scalar1=0.0)
+                nc.vector.tensor_scalar(
+                    out=row, in0=row, scalar1=0.0, scalar2=None, op0=ALU.max, op1=ALU.add, accum_out=total
+                )
+
+        def split_ksum(h):
+            ksum = kept["ksum", h]
+            pieces = double.tile([P, ROWS, PIECES], BF16, name="ksum_pieces")
+            rest1 = double.tile([P, ROWS], F32, name="rest1")
+            rest2 = double.tile([P, ROWS], F32, name="rest2")
+            nc.gpsimd.tensor_copy(out=pieces[:, :, 0], in_=ksum[:])
+            nc.gpsimd.tensor_tensor(out=rest1[:], in0=ksum[:], in1=pieces[:, :, 0], op=ALU.subtract)
+            nc.gpsimd.tensor_copy(out=pieces[:, :, 1], in_=rest1[:])
+            nc.gpsimd.tensor_tensor(out=rest2[:], in0=rest1[:], in1=pieces[:, :, 1], op=ALU.subtract)
+            nc.gpsimd.tensor_copy(out=pieces[:, :, 2], in_=rest2[:])
+            kept["ksum_pieces", h] = pieces
 
         def transpose_row(name, h, t):
             words = kept[name, h][:].bitcast(F32)
@@ -123,126 +109,81 @@ def tile_relu_linear_att_pa_kernel(tc, q, k, v, out):
             )
 
         def transposes(step):
-            k_ok, v_ok = valid(step + K_AHEAD), valid(step + V_AHEAD)
-            if not (k_ok or v_ok):
-                return
+            rows = [("k", step + K_AHEAD), ("v", step + V_AHEAD)]
             grouped = quad.tile([P, 2 * TOK], BF16, name="grouped", align_bytes=64)
+            flipped = [transpose_row(name, *divmod(i, ROWS)) if valid(i) else None for name, i in rows]
+            for side in range(2):
+                if valid(rows[side][1]):
+                    group_row(flipped[side], grouped, side)
             kept["grouped", step] = grouped
-            if k_ok:
-                flipped_k = transpose_row("k", *divmod(step + K_AHEAD, ROWS))
-            if v_ok:
-                flipped_v = transpose_row("v", *divmod(step + V_AHEAD, ROWS))
-            if k_ok:
-                group_row(flipped_k, grouped, 0)
-            if v_ok:
-                group_row(flipped_v, grouped, 1)
 
         def quantise_rows(step):
-            k_ok, v_ok = valid(step + K_AHEAD), valid(step + V_AHEAD)
-            if not (k_ok or v_ok):
+            k_there, v_there = valid(step + K_AHEAD), valid(step + V_AHEAD)
+            if not (k_there or v_there):
                 return
-            codes = codes_pool.tile([P, BANK], U32, name="codes", align_bytes=64)
-            scales = codes_pool.tile([P, BANK], U8, name="scales", align_bytes=64)
-            lo = 0 if k_ok else BANK // 2
-            hi = BANK if v_ok else BANK // 2
+            codes = row_codes.tile([P, BANK], U32, name="codes", align_bytes=64)
+            scales = row_codes.tile([P, BANK], U8, name="scales", align_bytes=64)
+            lo = 0 if k_there else BANK // 2
+            hi = BANK if v_there else BANK // 2
             nc.vector.quantize_mx(
                 out=codes[:, lo:hi].bitcast(FP8X4),
                 scales=scales[:, lo:hi],
                 in_=kept["grouped", step][:, lo * PACK : hi * PACK],
             )
-            if k_ok:
-                kept["k_codes", step + K_AHEAD] = (codes, scales)
-            if v_ok:
-                kept["v_codes", step + V_AHEAD] = (codes, scales)
-
-        def sum_k(h, t):
-            if rows_of(h)[t] != "P":
-                return
-            grouped = kept["grouped", ROWS * h + t - K_AHEAD]
-            for i in range(PASSES * PACK):
-                first = (i // PACK) * P * PACK + i % PACK
-                nc.tensor.matmul(
-                    out=ksum_ps(h)[:, t : t + 1],
-                    lhsT=grouped[:, first : first + P * PACK - PACK + 1 : PACK],
-                    rhs=ones[:],
-                    start=(i == 0),
-                    stop=(i == PASSES * PACK - 1),
-                )
-
-        def split_ksum(h):
-            ksum = kept["ksum", h]
-            n_pe = rows_of(h).count("P")
-            pieces = double.tile([P, ROWS, PIECES], BF16, name="ksum_pieces")
-            rest1 = double.tile([P, ROWS], F32, name="rest1")
-            rest2 = double.tile([P, ROWS], F32, name="rest2")
-            if n_pe:
-                nc.scalar.copy(out=ksum[:, :n_pe], in_=ksum_ps(h)[:, :n_pe])
-            nc.gpsimd.tensor_copy(out=pieces[:, :, 0], in_=ksum[:])
-            nc.gpsimd.tensor_tensor(out=rest1[:], in0=ksum[:], in1=pieces[:, :, 0], op=ALU.subtract)
-            nc.gpsimd.tensor_copy(out=pieces[:, :, 1], in_=rest1[:])
-            nc.gpsimd.tensor_tensor(out=rest2[:], in0=rest1[:], in1=pieces[:, :, 1], op=ALU.subtract)
-            nc.gpsimd.tensor_copy(out=pieces[:, :, 2], in_=rest2[:])
-            kept["ksum_pieces", h] = pieces
+            kept["k_codes", step + K_AHEAD] = codes, scales
+            kept["v_codes", step + V_AHEAD] = codes, scales
 
         def group_q(h, j):
             if j == 0:
                 kept["q_grouped", h] = double.tile([P, TOK * PACK], BF16, name="q_grouped", align_bytes=64)
-            n_pieces = G_PIECES if Q_ENG[h][j] == "G" else 1
-            width = Q_CHUNK // n_pieces
-            for i in range(n_pieces):
-                group_tokens(h, Q_ENG[h][j], j * Q_CHUNK + i * width, width)
-
-        def group_tokens(h, engine, first, width):
-            dst = kept["q_grouped", h][:, first * PACK : (first + width) * PACK].rearrange("p (c i t) -> p c t i", i=4, t=PACK)
-            source = kept["q", h][:].rearrange("p (t n) -> p t n", t=ROWS)[:, :, first : first + width].rearrange(
-                "p t (c i) -> p c t i", i=4
-            )
-            if engine == "S":
-                nc.scalar.activation(out=dst, in_=source, func=ACT.Relu)
-            elif engine == "G":
-                nc.gpsimd.tensor_scalar(out=dst, in0=source, scalar1=BIG, scalar2=0.0, op0=ALU.min, op1=ALU.max)
-            else:
-                nc.vector.tensor_scalar_max(out=dst, in0=source, scalar1=0.0)
+            engine = Q_ENGINE[h][j]
+            pieces = G_PIECES if engine == "G" else 1
+            width = CHUNK // pieces
+            for i in range(pieces):
+                first = j * CHUNK + i * width
+                dst = kept["q_grouped", h][:, first * PACK : (first + width) * PACK].rearrange(
+                    "p (c i t) -> p c t i", i=4, t=PACK
+                )
+                source = kept["q", h][:].rearrange("p (t n) -> p t n", t=ROWS)[:, :, first : first + width].rearrange(
+                    "p t (c i) -> p c t i", i=4
+                )
+                if engine == "S":
+                    nc.scalar.activation(out=dst, in_=source, func=ACT.Relu)
+                elif engine == "G":
+                    nc.gpsimd.tensor_scalar(out=dst, in0=source, scalar1=LARGEST, scalar2=0.0, op0=ALU.min, op1=ALU.max)
+                else:
+                    nc.vector.tensor_scalar_max(out=dst, in0=source, scalar1=0.0)
 
         def quantise_q(h):
-            kept["q_codes", h] = triple.tile([P, TOK], U32, name="q_codes", align_bytes=64)
-            kept["q_scales", h] = triple.tile([P, TOK], U8, name="q_scales", align_bytes=64)
+            kept["q_codes", h] = double.tile([P, TOK], U32, name="q_codes", align_bytes=64)
+            kept["q_scales", h] = double.tile([P, TOK], U8, name="q_scales", align_bytes=64)
             nc.vector.quantize_mx(
                 out=kept["q_codes", h][:].bitcast(FP8X4), scales=kept["q_scales", h][:], in_=kept["q_grouped", h][:]
             )
 
-        def den_matmuls(h, tiles):
-            for j in tiles:
+        def den_matmuls(h, half):
+            if half == 0:
+                kept["den_ps", h] = psum_den.tile([P, TOK_TILES, PIECES], F32, name="den_ps")
+            for j in range(half * TOK_TILES // 2, (half + 1) * TOK_TILES // 2):
                 for t in range(ROWS):
-                    first = (j * PACK if h >= DMA_FROM else j * P * PACK) + t
-                    apart = TOK_TILES * PACK if h >= DMA_FROM else PACK
+                    first = j * P * PACK + t
                     nc.tensor.matmul(
-                        out=den_ps(h)[:, j, :],
-                        lhsT=kept["q_grouped", h][:, first : first + (P - 1) * apart + 1 : apart],
+                        out=kept["den_ps", h][:, j, :],
+                        lhsT=kept["q_grouped", h][:, first : first + P * PACK - PACK + 1 : PACK],
                         rhs=kept["ksum_pieces", h][:, t, :],
                         start=(t == 0),
                         stop=(t == ROWS - 1),
                     )
 
         def reciprocal_den(h):
+            den = double.tile([P, TOK_TILES], F32, name="den")
             rden = double.tile([P, TOK_TILES], F32, name="rden")
-            nc.vector.reciprocal(out=rden[:], in_=kept["den", h][:])
+            nc.vector.tensor_reduce(out=den[:], in_=kept["den_ps", h][:], axis=mybir.AxisListType.X, op=ALU.add)
+            nc.vector.reciprocal(out=rden[:], in_=den[:])
             kept["rden", h] = rden
 
-        def reduce_den(h):
-            den = double.tile([P, TOK_TILES], F32, name="den")
-            nc.vector.tensor_reduce(out=den[:], in_=den_ps(h), axis=mybir.AxisListType.X, op=ALU.add)
-            kept["den", h] = den
-
         def spread_rden(h):
-            kept["rden_rows", h] = triple.tile([P, TOK], F32, name="rden_rows")
-            if h >= DMA_FROM:
-                row = out[0, (FEAT - 1) * 2 + h // 2, (h % 2) * TOK : (h % 2 + 1) * TOK]
-                nc.sync.dma_start(out=row.rearrange("(p j) -> p j", j=TOK_TILES), in_=kept["rden", h][:])
-                nc.sync.dma_start(out=kept["rden_rows", h][:], in_=row.partition_broadcast(P))
-                if h == DMA_FROM:
-                    load_list(LOADS2)
-                return
+            kept["rden_rows", h] = double.tile([P, TOK], F32, name="rden_rows")
             for half in range(HALVES):
                 spread = psum.tile([P, BANK], F32, name="spread", tag="bank")
                 for jj in range(BANK // P):
@@ -272,7 +213,7 @@ def tile_relu_linear_att_pa_kernel(tc, q, k, v, out):
             kept["vk_ps", h, c] = vk_ps
 
         def round_vk(h, c):
-            vk_grouped = triple.tile([P, P * PACK], BF16, name="vk_grouped", align_bytes=64)
+            vk_grouped = double.tile([P, P * PACK], BF16, name="vk_grouped", align_bytes=64)
             nc.scalar.copy(
                 out=vk_grouped[:].rearrange("p (j t) -> p j t", t=PACK),
                 in_=kept["vk_ps", h, c][:].rearrange("p (t j) -> p j t", t=ROWS),
@@ -280,8 +221,8 @@ def tile_relu_linear_att_pa_kernel(tc, q, k, v, out):
             kept["vk_grouped", h, c] = vk_grouped
 
         def quantise_vk(h, c):
-            kept["vk_codes", h, c] = vk_pool.tile([P, P], U32, name="vk_codes", align_bytes=64)
-            kept["vk_scales", h, c] = vk_pool.tile([P, P], U8, name="vk_scales", align_bytes=64)
+            kept["vk_codes", h, c] = triple.tile([P, P], U32, name="vk_codes", align_bytes=64)
+            kept["vk_scales", h, c] = triple.tile([P, P], U8, name="vk_scales", align_bytes=64)
             nc.vector.quantize_mx(
                 out=kept["vk_codes", h, c][:].bitcast(FP8X4),
                 scales=kept["vk_scales", h, c][:],
@@ -312,59 +253,49 @@ def tile_relu_linear_att_pa_kernel(tc, q, k, v, out):
                 )
                 nc.sync.dma_start(out=out_view[:, c, h // 2, h % 2, n_cols], in_=result[:])
 
-        every = slice(0, ROWS)
-        all_tok = slice(0, TOK)
-        src = {"k": k, "q": q, "v": v}
-
-        def load_list(items):
-            for item in items.split():
-                nm = item[0]
-                hd = int(item[1])
-                rows = slice(int(item[2]), int(item[-1]) + 1) if len(item) > 2 else every
-                load(nm, src[nm], hd, rows, all_tok)
-
-        load_list(LOADS)
-
         def valid(quarter):
             return 0 <= quarter < QUARTERS
 
+        pair = ROWS // 2
+        for t in range(ROWS):
+            load("k", k, 0, t, 1)
+        for h in range(HEADS):
+            for first in range(0, ROWS, pair):
+                if h + 1 < HEADS:
+                    load("k", k, h + 1, first, pair)
+                if first == 0:
+                    load("q", q, h, 0, ROWS)
+                load("v", v, h, first, pair)
+
         for step in range(-RELU_AHEAD, QUARTERS + BEHIND):
-            for stage in ORDER:
-                if stage == "R" and valid(step + RELU_AHEAD):
-                    relu_k(*divmod(step + RELU_AHEAD, ROWS))
-                if stage == "T":
-                    if step < PAIR_FROM:
-                        transposes(step)
-                    elif step % 2 == 0:
-                        transposes(step)
-                        transposes(step + 1)
-                if stage == "K":
-                    quantise_rows(step - 1)
-                if stage == "M" and valid(step - BEHIND):
-                    second_matmul(*divmod(step - BEHIND, ROWS))
-                if stage == "U" and valid(step - 1):
-                    quantise_vk(*divmod(step - 1, ROWS))
-                if stage == "G" and valid(step + Q_AHEAD):
-                    group_q(*divmod(step + Q_AHEAD, ROWS))
-                if stage == "F" and valid(step):
-                    first_matmul(*divmod(step, ROWS))
-                if stage == "C" and valid(step):
-                    round_vk(*divmod(step, ROWS))
-                if stage == "S" and valid(step + KSUM_AHEAD):
-                    sum_k(*divmod(step + KSUM_AHEAD, ROWS))
-                    if (step + KSUM_AHEAD) % ROWS == ROWS - 1:
-                        split_ksum((step + KSUM_AHEAD) // ROWS)
-                if stage == "Q" and valid(step - QQ_STEP) and (step - QQ_STEP) % ROWS == 0:
-                    quantise_q((step - QQ_STEP) // ROWS)
-                if stage == "D":
-                    for i in range(2):
-                        if valid(step - DEN_STEPS[i]) and (step - DEN_STEPS[i]) % ROWS == 0:
-                            den_matmuls((step - DEN_STEPS[i]) // ROWS, range(i * TOK_TILES // 2, (i + 1) * TOK_TILES // 2))
-                if stage == "V" and valid(step - BEHIND):
-                    divide_and_store(*divmod(step - BEHIND, ROWS))
-                if stage == "Z" and valid(step - RDEN_STEP) and (step - RDEN_STEP) % ROWS == 0:
-                    reduce_den((step - RDEN_STEP) // ROWS)
-                if stage == "X" and valid(step - RDEN_STEP) and (step - RDEN_STEP) % ROWS == 0:
-                    reciprocal_den((step - RDEN_STEP) // ROWS)
-                if stage == "Y" and valid(step - RDEN_STEP) and (step - RDEN_STEP) % ROWS == 0:
-                    spread_rden((step - RDEN_STEP) // ROWS)
+            head, c = divmod(step, ROWS)
+            if valid(step) and c == 1:
+                reciprocal_den(head)
+            if valid(step - BEHIND):
+                second_matmul(*divmod(step - BEHIND, ROWS))
+                divide_and_store(*divmod(step - BEHIND, ROWS))
+            quantise_rows(step - 1)
+            if valid(step) and c == 0:
+                quantise_q(head)
+            if valid(step - 1):
+                quantise_vk(*divmod(step - 1, ROWS))
+            if valid(step + RELU_AHEAD):
+                relu_k(*divmod(step + RELU_AHEAD, ROWS))
+            if valid(step + 2) and c == 2:
+                split_ksum(head + 1)
+            if valid(step + Q_AHEAD):
+                group_q(*divmod(step + Q_AHEAD, ROWS))
+            if step < 0:
+                transposes(step)
+            elif step % 2 == 0:
+                transposes(step)
+                transposes(step + 1)
+            if valid(step + 1) and c == ROWS - 1:
+                den_matmuls(head + 1, 0)
+            if valid(step):
+                if c == 0:
+                    den_matmuls(head, 1)
+                first_matmul(head, c)
+                round_vk(head, c)
+                if c == 1:
+                    spread_rden(head)

@@ -34,9 +34,9 @@ QUARTERS = HEADS * ROWS
 
 FLOPS = 2 * 2 * HEADS * FEAT * FEAT * TOK
 
-ROW_ENGINE = "VVVS"
+ROW_ENGINE = ('VVVS', 'VSVS', 'VVVS', 'VSVS')
 Q_ENGINE = ("VVVV", "GVGS", "GVGS", "GSGS")
-G_PIECES = 2
+G_PIECES = 1
 
 
 def tile_relu_linear_att_pa_kernel(tc, q, k, v, out):
@@ -73,7 +73,7 @@ def tile_relu_linear_att_pa_kernel(tc, q, k, v, out):
                 kept["ksum", h] = double.tile([P, ROWS], F32, name="ksum")
             row = kept["k", h][:, t * TOK : (t + 1) * TOK]
             total = kept["ksum", h][:, t : t + 1]
-            if ROW_ENGINE[t] == "S":
+            if ROW_ENGINE[h][t] == "S":
                 nc.scalar.activation(out=row, in_=row, func=ACT.Relu, accum_out=total)
             else:
                 nc.vector.tensor_scalar(
@@ -177,8 +177,12 @@ def tile_relu_linear_att_pa_kernel(tc, q, k, v, out):
 
         def reciprocal_den(h):
             den = double.tile([P, TOK_TILES], F32, name="den")
-            rden = double.tile([P, TOK_TILES], F32, name="rden")
             nc.vector.tensor_reduce(out=den[:], in_=kept["den_ps", h][:], axis=mybir.AxisListType.X, op=ALU.add)
+            kept["den", h] = den
+
+        def invert_den(h):
+            rden = double.tile([P, TOK_TILES], F32, name="rden")
+            den = kept["den", h]
             nc.vector.reciprocal(out=rden[:], in_=den[:])
             kept["rden", h] = rden
 
@@ -274,6 +278,8 @@ def tile_relu_linear_att_pa_kernel(tc, q, k, v, out):
             if valid(step - BEHIND):
                 second_matmul(*divmod(step - BEHIND, ROWS))
                 divide_and_store(*divmod(step - BEHIND, ROWS))
+            if valid(step) and c == 1:
+                invert_den(head)
             quantise_rows(step - 1)
             if valid(step) and c == 0:
                 quantise_q(head)
@@ -285,6 +291,8 @@ def tile_relu_linear_att_pa_kernel(tc, q, k, v, out):
                 split_ksum(head + 1)
             if valid(step + Q_AHEAD):
                 group_q(*divmod(step + Q_AHEAD, ROWS))
+            if valid(step) and c == 2:
+                spread_rden(head)
             if step < 0:
                 transposes(step)
             elif step % 2 == 0:
@@ -297,5 +305,3 @@ def tile_relu_linear_att_pa_kernel(tc, q, k, v, out):
                     den_matmuls(head, 1)
                 first_matmul(head, c)
                 round_vk(head, c)
-                if c == 1:
-                    spread_rden(head)

@@ -34,7 +34,7 @@ QUARTERS = HEADS * ROWS
 
 FLOPS = 2 * 2 * HEADS * FEAT * FEAT * TOK
 
-ROW_ENGINE = ('VVVS', 'VSVS', 'VVVS', 'VSVS')
+ROW_ENGINE = "VSVS"
 Q_ENGINE = ("VVVV", "GVGS", "GVGS", "GSGS")
 G_PIECES = 1
 
@@ -73,7 +73,7 @@ def tile_relu_linear_att_pa_kernel(tc, q, k, v, out):
                 kept["ksum", h] = double.tile([P, ROWS], F32, name="ksum")
             row = kept["k", h][:, t * TOK : (t + 1) * TOK]
             total = kept["ksum", h][:, t : t + 1]
-            if ROW_ENGINE[h][t] == "S":
+            if ROW_ENGINE[t] == "S":
                 nc.scalar.activation(out=row, in_=row, func=ACT.Relu, accum_out=total)
             else:
                 nc.vector.tensor_scalar(

from contextlib import ExitStack

import concourse.mybir as mybir
from concourse.masks import make_identity

F32 = mybir.dt.float32
BF16 = mybir.dt.bfloat16
U32 = mybir.dt.uint32
U8 = mybir.dt.uint8
FP8X4 = mybir.dt.float8_e4m3fn_x4
ALU = mybir.AluOpType
ACT = mybir.ActivationFunctionType

P = 128
PACK = 4
HEADS = 4
FEAT = 512
TOK = 1024
ROWS = FEAT // P
PASSES = TOK // (P * PACK)
BANK = 512
HALVES = TOK // BANK
TOK_TILES = TOK // P
PIECES = 3
CHUNK = TOK // ROWS
LARGEST = 3.3895313892515355e38

RELU_AHEAD = 8
K_AHEAD = 6
Q_AHEAD = 4
V_AHEAD = 2
BEHIND = 3
QUARTERS = HEADS * ROWS

FLOPS = 2 * 2 * HEADS * FEAT * FEAT * TOK

ROW_ENGINE = "VSVS"
Q_ENGINE = ("VVVV", "GVGS", "GVGS", "GSGS")
G_PIECES = 1


def tile_relu_linear_att_pa_kernel(tc, q, k, v, out):
    nc = tc.nc
    out_view = out[0].rearrange("(j c a) (b n) -> j c a b n", c=ROWS, a=2, b=2)

    with ExitStack() as ctx:
        consts = ctx.enter_context(tc.tile_pool(name="consts", bufs=1))
        inputs = ctx.enter_context(tc.tile_pool(name="inputs", bufs=HEADS))
        double = ctx.enter_context(tc.tile_pool(name="double", bufs=2))
        triple = ctx.enter_context(tc.tile_pool(name="triple", bufs=3))
        quad = ctx.enter_context(tc.tile_pool(name="quad", bufs=4))
        row_codes = ctx.enter_context(tc.tile_pool(name="row_codes", bufs=10))
        results = ctx.enter_context(tc.tile_pool(name="results", bufs=8))
        psum = ctx.enter_context(tc.psum_pool(name="psum", bufs=7))
        psum_den = ctx.enter_context(tc.psum_pool(name="psum_den", bufs=1))
        ctx.enter_context(tc.manual_schedule())

        identity = consts.tile([P, P], F32)
        make_identity(nc, identity[:])

        kept = {}

        def load(name, src, h, first_row, n_rows):
            if (name, h) not in kept:
                kept[name, h] = inputs.tile([P, ROWS * TOK], BF16, name=name + "_rows")
            cols = slice(first_row * TOK, (first_row + n_rows) * TOK)
            nc.sync.dma_start(
                out=kept[name, h][:, cols], in_=src[0, h].rearrange("(p t) n -> p (t n)", t=ROWS)[:, cols]
            )

        def relu_k(h, t):
            if t == 0:
                kept["ksum", h] = double.tile([P, ROWS], F32, name="ksum")
            row = kept["k", h][:, t * TOK : (t + 1) * TOK]
            total = kept["ksum", h][:, t : t + 1]
            if ROW_ENGINE[t] == "S":
                nc.scalar.activation(out=row, in_=row, func=ACT.Relu, accum_out=total)
            else:
                nc.vector.tensor_scalar(
                    out=row, in0=row, scalar1=0.0, scalar2=None, op0=ALU.max, op1=ALU.add, accum_out=total
                )

        def split_ksum(h):
            ksum = kept["ksum", h]
            pieces = double.tile([P, ROWS, PIECES], BF16, name="ksum_pieces")
            rest1 = double.tile([P, ROWS], F32, name="rest1")
            rest2 = double.tile([P, ROWS], F32, name="rest2")
            nc.gpsimd.tensor_copy(out=pieces[:, :, 0], in_=ksum[:])
            nc.gpsimd.tensor_tensor(out=rest1[:], in0=ksum[:], in1=pieces[:, :, 0], op=ALU.subtract)
            nc.gpsimd.tensor_copy(out=pieces[:, :, 1], in_=rest1[:])
            nc.gpsimd.tensor_tensor(out=rest2[:], in0=rest1[:], in1=pieces[:, :, 1], op=ALU.subtract)
            nc.gpsimd.tensor_copy(out=pieces[:, :, 2], in_=rest2[:])
            kept["ksum_pieces", h] = pieces

        def transpose_row(name, h, t):
            words = kept[name, h][:].bitcast(F32)
            flipped = psum.tile([P, BANK], F32, name="flipped", tag="bank")
            for b in range(ROWS):
                first = t * (TOK // 2) + b * P
                nc.tensor.transpose(flipped[:, b * P : (b + 1) * P], words[:, first : first + P], identity[:])
            return flipped

        def group_row(flipped, grouped, side):
            nc.scalar.copy(
                out=grouped[:].bitcast(F32)[:, side * BANK : (side + 1) * BANK].rearrange(
                    "p (g c u) -> p g c u", g=PASSES, u=2
                ),
                in_=flipped[:].rearrange("p (g u c) -> p g c u", g=PASSES, u=2),
            )

        def transposes(step):
            rows = [("k", step + K_AHEAD), ("v", step + V_AHEAD)]
            grouped = quad.tile([P, 2 * TOK], BF16, name="grouped", align_bytes=64)
            flipped = [transpose_row(name, *divmod(i, ROWS)) if valid(i) else None for name, i in rows]
            for side in range(2):
                if valid(rows[side][1]):
                    group_row(flipped[side], grouped, side)
            kept["grouped", step] = grouped

        def quantise_rows(step):
            k_there, v_there = valid(step + K_AHEAD), valid(step + V_AHEAD)
            if not (k_there or v_there):
                return
            codes = row_codes.tile([P, BANK], U32, name="codes", align_bytes=64)
            scales = row_codes.tile([P, BANK], U8, name="scales", align_bytes=64)
            lo = 0 if k_there else BANK // 2
            hi = BANK if v_there else BANK // 2
            nc.vector.quantize_mx(
                out=codes[:, lo:hi].bitcast(FP8X4),
                scales=scales[:, lo:hi],
                in_=kept["grouped", step][:, lo * PACK : hi * PACK],
            )
            kept["k_codes", step + K_AHEAD] = codes, scales
            kept["v_codes", step + V_AHEAD] = codes, scales

        def group_q(h, j):
            if j == 0:
                kept["q_grouped", h] = double.tile([P, TOK * PACK], BF16, name="q_grouped", align_bytes=64)
            engine = Q_ENGINE[h][j]
            pieces = G_PIECES if engine == "G" else 1
            width = CHUNK // pieces
            for i in range(pieces):
                first = j * CHUNK + i * width
                dst = kept["q_grouped", h][:, first * PACK : (first + width) * PACK].rearrange(
                    "p (c i t) -> p c t i", i=4, t=PACK
                )
                source = kept["q", h][:].rearrange("p (t n) -> p t n", t=ROWS)[:, :, first : first + width].rearrange(
                    "p t (c i) -> p c t i", i=4
                )
                if engine == "S":
                    nc.scalar.activation(out=dst, in_=source, func=ACT.Relu)
                elif engine == "G":
                    nc.gpsimd.tensor_scalar(out=dst, in0=source, scalar1=LARGEST, scalar2=0.0, op0=ALU.min, op1=ALU.max)
                else:
                    nc.vector.tensor_scalar_max(out=dst, in0=source, scalar1=0.0)

        def quantise_q(h):
            kept["q_codes", h] = double.tile([P, TOK], U32, name="q_codes", align_bytes=64)
            kept["q_scales", h] = double.tile([P, TOK], U8, name="q_scales", align_bytes=64)
            nc.vector.quantize_mx(
                out=kept["q_codes", h][:].bitcast(FP8X4), scales=kept["q_scales", h][:], in_=kept["q_grouped", h][:]
            )

        def den_matmuls(h, half):
            if half == 0:
                kept["den_ps", h] = psum_den.tile([P, TOK_TILES, PIECES], F32, name="den_ps")
            for j in range(half * TOK_TILES // 2, (half + 1) * TOK_TILES // 2):
                for t in range(ROWS):
                    first = j * P * PACK + t
                    nc.tensor.matmul(
                        out=kept["den_ps", h][:, j, :],
                        lhsT=kept["q_grouped", h][:, first : first + P * PACK - PACK + 1 : PACK],
                        rhs=kept["ksum_pieces", h][:, t, :],
                        start=(t == 0),
                        stop=(t == ROWS - 1),
                    )

        def reciprocal_den(h):
            den = double.tile([P, TOK_TILES], F32, name="den")
            nc.vector.tensor_reduce(out=den[:], in_=kept["den_ps", h][:], axis=mybir.AxisListType.X, op=ALU.add)
            kept["den", h] = den

        def invert_den(h):
            rden = double.tile([P, TOK_TILES], F32, name="rden")
            den = kept["den", h]
            nc.vector.reciprocal(out=rden[:], in_=den[:])
            kept["rden", h] = rden

        def spread_rden(h):
            kept["rden_rows", h] = double.tile([P, TOK], F32, name="rden_rows")
            for half in range(HALVES):
                spread = psum.tile([P, BANK], F32, name="spread", tag="bank")
                for jj in range(BANK // P):
                    j = half * (BANK // P) + jj
                    nc.tensor.transpose(
                        spread[:, jj * P : (jj + 1) * P], kept["rden", h][:, j : j + 1].to_broadcast([P, P]), identity[:]
                    )
                nc.scalar.copy(out=kept["rden_rows", h][:, half * BANK : (half + 1) * BANK], in_=spread[:])

        def first_matmul(h, c):
            vk_ps = psum.tile([P, BANK], F32, name="vk_ps", tag="bank")
            v_codes, v_scales = kept["v_codes", ROWS * h + c]
            for t in range(ROWS):
                k_codes, k_scales = kept["k_codes", ROWS * h + t]
                for g in range(PASSES):
                    k_cols = slice(g * P, (g + 1) * P)
                    v_cols = slice(BANK // 2 + g * P, BANK // 2 + (g + 1) * P)
                    nc.tensor.matmul_mx(
                        out=vk_ps[:, t * P : (t + 1) * P],
                        lhsT=k_codes[:, k_cols].bitcast(FP8X4),
                        lhsT_scale=k_scales[:, k_cols],
                        rhs=v_codes[:, v_cols].bitcast(FP8X4),
                        rhs_scale=v_scales[:, v_cols],
                        start=(g == 0),
                        stop=(g == PASSES - 1),
                    )
            kept["vk_ps", h, c] = vk_ps

        def round_vk(h, c):
            vk_grouped = double.tile([P, P * PACK], BF16, name="vk_grouped", align_bytes=64)
            nc.scalar.copy(
                out=vk_grouped[:].rearrange("p (j t) -> p j t", t=PACK),
                in_=kept["vk_ps", h, c][:].rearrange("p (t j) -> p j t", t=ROWS),
            )
            kept["vk_grouped", h, c] = vk_grouped

        def quantise_vk(h, c):
            kept["vk_codes", h, c] = triple.tile([P, P], U32, name="vk_codes", align_bytes=64)
            kept["vk_scales", h, c] = triple.tile([P, P], U8, name="vk_scales", align_bytes=64)
            nc.vector.quantize_mx(
                out=kept["vk_codes", h, c][:].bitcast(FP8X4),
                scales=kept["vk_scales", h, c][:],
                in_=kept["vk_grouped", h, c][:],
            )

        def second_matmul(h, c):
            for half in range(HALVES):
                n_cols = slice(half * BANK, (half + 1) * BANK)
                num_ps = psum.tile([P, BANK], F32, name="num_ps", tag="bank")
                nc.tensor.matmul_mx(
                    out=num_ps[:],
                    lhsT=kept["vk_codes", h, c][:].bitcast(FP8X4),
                    lhsT_scale=kept["vk_scales", h, c][:],
                    rhs=kept["q_codes", h][:, n_cols].bitcast(FP8X4),
                    rhs_scale=kept["q_scales", h][:, n_cols],
                    start=True,
                    stop=True,
                )
                kept["num_ps", h, c, half] = num_ps

        def divide_and_store(h, c):
            for half in range(HALVES):
                n_cols = slice(half * BANK, (half + 1) * BANK)
                result = results.tile([P, BANK], F32, name="result")
                nc.vector.tensor_tensor(
                    out=result[:], in0=kept["num_ps", h, c, half][:], in1=kept["rden_rows", h][:, n_cols], op=ALU.mult
                )
                nc.sync.dma_start(out=out_view[:, c, h // 2, h % 2, n_cols], in_=result[:])

        def valid(quarter):
            return 0 <= quarter < QUARTERS

        pair = ROWS // 2
        for t in range(ROWS):
            load("k", k, 0, t, 1)
        for h in range(HEADS):
            for first in range(0, ROWS, pair):
                if h + 1 < HEADS:
                    load("k", k, h + 1, first, pair)
                if first == 0:
                    load("q", q, h, 0, ROWS)
                load("v", v, h, first, pair)

        for step in range(-RELU_AHEAD, QUARTERS + BEHIND):
            head, c = divmod(step, ROWS)
            if valid(step) and c == 1:
                reciprocal_den(head)
            if valid(step - BEHIND):
                second_matmul(*divmod(step - BEHIND, ROWS))
                divide_and_store(*divmod(step - BEHIND, ROWS))
            if valid(step) and c == 1:
                invert_den(head)
            quantise_rows(step - 1)
            if valid(step) and c == 0:
                quantise_q(head)
            if valid(step - 1):
                quantise_vk(*divmod(step - 1, ROWS))
            if valid(step + RELU_AHEAD):
                relu_k(*divmod(step + RELU_AHEAD, ROWS))
            if valid(step + 2) and c == 2:
                split_ksum(head + 1)
            if valid(step + Q_AHEAD):
                group_q(*divmod(step + Q_AHEAD, ROWS))
            if valid(step) and c == 2:
                spread_rden(head)
            if step < 0:
                transposes(step)
            elif step % 2 == 0:
                transposes(step)
                transposes(step + 1)
            if valid(step + 1) and c == ROWS - 1:
                den_matmuls(head + 1, 0)
            if valid(step):
                if c == 0:
                    den_matmuls(head, 1)
                first_matmul(head, c)
                round_vk(head, c)
